import numpy as np
import ml_dtypes


def mxq(x, axis, fmt="e4m3"):
    dtype, down = {"e4m3": (ml_dtypes.float8_e4m3fn, 7), "e5m2": (ml_dtypes.float8_e5m2, 14)}[fmt]
    v = np.moveaxis(np.asarray(x, np.float32).astype(ml_dtypes.bfloat16).astype(np.float64), axis, -1)
    blocks = v.reshape(v.shape[:-1] + (-1, 32))
    amax = np.abs(blocks).max(-1, keepdims=True)
    byte = np.maximum(np.where(amax > 0, np.frexp(amax)[1] - 1 + 127, 0) - down, 1)
    scale = np.exp2(byte - 127.0)
    codes = (blocks / scale).astype(np.float32).astype(dtype).astype(np.float64)
    return np.moveaxis((codes * scale).reshape(v.shape), -1, axis)


WIDE = False


def mx_kscale(k):
    if not WIDE:
        return np.ones(k)
    levels = np.array([10, -10, 5, -5, 0])
    a = np.random.permutation(np.resize(levels, k // 512 * 4)).reshape(k // 512, 4)
    idx = np.arange(k)
    return np.exp2(a[idx // 512, idx % 128 // 32])


BF16 = ml_dtypes.bfloat16


def bf(x):
    return np.asarray(x, np.float32).astype(BF16)


def f64(x):
    return np.asarray(x).astype(np.float64)


R, C, B, E, H = 16, 512, 1, 512, 8
D = E // H


def setup_inputs():
    s, t = mx_kscale(E), mx_kscale(E)
    return {"x": bf(np.random.standard_normal((R, C, B, E)) * s),
            "Wq": bf(np.random.standard_normal((E, E)) * 1.4 / np.sqrt(E) / s[:, None] * t),
            "bq": bf(np.random.standard_normal(E) * 0.3 * t),
            "k": bf(np.random.standard_normal((R, C, B, H, D)) * 1.4 / t.reshape(H, D))}


def reference(x, Wq, bq, k):
    scaling = D ** -0.5 / np.sqrt(R)
    q = ((mxq(f64(x), 3, "e4m3") @ mxq(f64(Wq), 0, "e4m3")) + f64(bq)) * scaling
    qh = q.reshape(R, C, B, H, D).transpose(3, 2, 1, 0, 4).reshape(H, B, C, R * D)
    kh = f64(k).transpose(3, 2, 0, 4, 1).reshape(H, B, R * D, C)
    sc = mxq(qh, 3, "e4m3") @ mxq(kh, 2, "e4m3")
    e = np.exp(sc - sc.max(-1, keepdims=True))
    return e / e.sum(-1, keepdims=True)

@@ -1,0 +1,314 @@
+from contextlib import ExitStack
+
+import concourse.mybir as mybir
+from concourse.masks import make_identity
+
+F32 = mybir.dt.float32
+BF16 = mybir.dt.bfloat16
+U32 = mybir.dt.uint32
+U8 = mybir.dt.uint8
+I32 = mybir.dt.int32
+FP8X4 = mybir.dt.float8_e4m3fn_x4
+ACT = mybir.ActivationFunctionType
+ALU = mybir.AluOpType
+
+P = 128
+PACK = 4
+BANK = 512
+ROWS, COLS, WIDTH, HEADS, HEAD_DIM = 16, 512, 512, 8, 64
+COL_TILES = COLS // P
+HALF_ROWS = 8
+HALVES = ROWS // HALF_ROWS
+HEAD_GROUP = 4
+SCALING = 1.0 / 32.0
+
+X_JOBS = COL_TILES * HALVES
+KEY_JOBS = HALVES * COL_TILES
+ROUNDS = COL_TILES * (HEADS // HEAD_GROUP) * HALVES
+ATTEND_FROM = KEY_JOBS + 1
+
+FLOPS = 2 * ROWS * COLS * WIDTH * WIDTH + 2 * HEADS * COLS * COLS * ROWS * HEAD_DIM
+
+
+def row_in_half(a, t):
+    return 4 * (t // 2) + 2 * a + (t % 2)
+
+
+def tile_rowselfattention_pa_t_kernel(tc, x, Wq, bq, k, out):
+    nc = tc.nc
+    x_view = x[:, :, 0, :].rearrange("r (t p) e -> p t r e", p=P)
+    k_view = k[:, :, 0].rearrange("r (t p) h d -> p t r (h d)", p=P)
+    out_view = out[:, 0].rearrange("h (t p) j -> p h t j", p=P)
+
+    with ExitStack() as ctx:
+        ctx.enter_context(tc.manual_schedule())
+        keep = ctx.enter_context(tc.tile_pool(name="keep", bufs=1))
+        k_in = ctx.enter_context(tc.tile_pool(name="k_in", bufs=3))
+        k_work = ctx.enter_context(tc.tile_pool(name="k_work", bufs=2))
+        x_in = ctx.enter_context(tc.tile_pool(name="x_in", bufs=3))
+        x_work = ctx.enter_context(tc.tile_pool(name="x_work", bufs=2))
+        x_mx = ctx.enter_context(tc.tile_pool(name="x_mx", bufs=4))
+        turn_psum = ctx.enter_context(tc.psum_pool(name="turn_psum", bufs=2))
+        acc_psum = ctx.enter_context(tc.psum_pool(name="acc_psum", bufs=6))
+
+        x_raw_of, x_grouped_of, x_mx_of = {}, {}, {}
+        k_raw_of, k_pairs_of, k_grouped_of = {}, {}, {}
+        q_grouped_of, q_mx_of = {}, {}
+        scores_of = {}
+
+        def load_x(job):
+            it, half = job // HALVES, job % HALVES
+            x_raw = x_in.tile([P, HALF_ROWS * WIDTH], BF16)
+            nc.sync.dma_start(
+                out=x_raw[:].rearrange("p (r e) -> p r e", r=HALF_ROWS),
+                in_=x_view[:, it, half * HALF_ROWS : (half + 1) * HALF_ROWS, :],
+            )
+            x_raw_of[job] = x_raw
+
+        def load_keys(job):
+            half, jt = job // COL_TILES, job % COL_TILES
+            k_raw = k_in.tile([P, HALF_ROWS * WIDTH], BF16)
+            nc.sync.dma_start(
+                out=k_raw[:].rearrange("p (r e) -> p r e", r=HALF_ROWS),
+                in_=k_view[:, jt, half * HALF_ROWS : (half + 1) * HALF_ROWS, :],
+            )
+            k_raw_of[job] = k_raw
+
+        def turn_x(job):
+            x_words = x_raw_of[job][:].bitcast(F32)
+            x_grouped = x_work.tile([P, HALF_ROWS * P * PACK], BF16, align_bytes=64)
+            x_grouped_words = x_grouped[:].bitcast(F32)
+            for bank in range(HALF_ROWS // 2):
+                turned = turn_psum.tile([P, 2, 2, P], F32, tag="turn")
+                for s2 in range(2):
+                    slot = 2 * bank + s2
+                    row = row_in_half(slot // PACK, slot % PACK)
+                    for u in range(2):
+                        first = row * (WIDTH // 2) + u * P
+                        nc.tensor.transpose(
+                            turned[:, s2, u, :], x_words[:, first : first + P], ident_f32[:]
+                        )
+                dst = x_grouped_words[:, bank * BANK : (bank + 1) * BANK].rearrange(
+                    "p (s i u) -> p s i u", s=2, u=2
+                )
+                src = turned[:].rearrange("p s u i -> p s i u")
+                if bank % 2 == 0:
+                    nc.vector.tensor_copy(out=dst, in_=src)
+                else:
+                    nc.scalar.copy(out=dst, in_=src)
+            x_grouped_of[job] = x_grouped
+
+        def quantise_x(job):
+            x_codes = x_mx.tile([P, HALF_ROWS * P], U32, align_bytes=64)
+            x_scales = x_mx.tile([P, HALF_ROWS * P], U8, align_bytes=64)
+            nc.vector.quantize_mx(
+                out=x_codes[:].bitcast(FP8X4), scales=x_scales[:], in_=x_grouped_of[job][:]
+            )
+            x_mx_of[job] = (x_codes, x_scales)
+
+        def pair_keys(job):
+            k_raw = k_raw_of[job]
+            k_pairs = k_work.tile([P, HALF_ROWS * WIDTH], BF16)
+            for u in range(2):
+                nc.vector.tensor_copy(
+                    out=k_pairs[:, u * 2048 : (u + 1) * 2048].rearrange(
+                        "p (h a d e) -> p h a d e", h=HEADS, a=2, e=2
+                    ),
+                    in_=k_raw[:, u * 2048 : (u + 1) * 2048].rearrange(
+                        "p (a e h d) -> p h a d e", a=2, e=2, h=HEADS
+                    ),
+                )
+            k_pairs_of[job] = k_pairs
+
+        def turn_keys(job):
+            k_words = k_pairs_of[job][:].bitcast(F32)
+            k_grouped = k_work.tile([P, HEADS * P * PACK], BF16, align_bytes=64)
+            k_grouped_words = k_grouped[:].bitcast(F32)
+            for bank in range(HEADS // 2):
+                turned = turn_psum.tile([P, 2, 2, P], F32, tag="turn")
+                for h2 in range(2):
+                    for u in range(2):
+                        first = (u * HEADS + 2 * bank + h2) * P
+                        nc.tensor.transpose(
+                            turned[:, h2, u, :], k_words[:, first : first + P], ident_f32[:]
+                        )
+                nc.scalar.copy(
+                    out=k_grouped_words[:, bank * BANK : (bank + 1) * BANK].rearrange(
+                        "p (h j u) -> p h j u", h=2, u=2
+                    ),
+                    in_=turned[:].rearrange("p h u j -> p h j u"),
+                )
+            k_grouped_of[job] = k_grouped
+
+        def quantise_keys(job):
+            half, jt = job // COL_TILES, job % COL_TILES
+            for h in range(HEADS):
+                first = (h * HALVES + half) * COLS + jt * P
+                nc.vector.quantize_mx(
+                    out=k_codes[:, first : first + P].bitcast(FP8X4),
+                    scales=k_scales[:, first : first + P],
+                    in_=k_grouped_of[job][:, h * P * PACK : (h + 1) * P * PACK],
+                )
+
+        def project_head(rnd, h4):
+            it, group, half = rnd // 4, (rnd % 4) // 2, rnd % 2
+            h = group * HEAD_GROUP + h4
+            x_codes, x_scales = x_mx_of[it * HALVES + half]
+            if h4 == 0:
+                q_grouped = q_work.tile([P, HEAD_GROUP * P * PACK], BF16, align_bytes=64)
+                q_grouped_of[rnd] = q_grouped
+            q_acc = acc_psum.tile([P, BANK], F32, tag="acc")
+            for a in range(2):
+                w_first = (2 * h + 1 - a) * HEAD_DIM
+                nc.tensor.matmul_mx(
+                    out=q_acc[:],
+                    lhsT=w_codes[:, w_first : w_first + P].bitcast(FP8X4),
+                    lhsT_scale=w_scales[:, w_first : w_first + P],
+                    rhs=x_codes[:, a * BANK : (a + 1) * BANK].bitcast(FP8X4),
+                    rhs_scale=x_scales[:, a * BANK : (a + 1) * BANK],
+                    start=(a == 0),
+                    stop=(a == 1),
+                )
+            nc.scalar.activation(
+                out=q_grouped_of[rnd][:, h4 * BANK : (h4 + 1) * BANK].rearrange(
+                    "p (i t) -> p i t", t=PACK
+                ),
+                in_=q_acc[:].rearrange("p (t i) -> p i t", t=PACK),
+                func=ACT.Identity,
+                bias=bias[:, h : h + 1],
+                scale=SCALING,
+            )
+
+        def quantise_q(rnd):
+            it, part = rnd // 4, rnd % 4
+            if part == 0:
+                q_codes = q_mx.tile([P, HALVES * HEADS * P], U32, align_bytes=64)
+                q_scales = q_mx.tile([P, HALVES * HEADS * P], U8, align_bytes=64)
+                q_mx_of[it] = (q_codes, q_scales)
+            q_codes, q_scales = q_mx_of[it]
+            nc.vector.quantize_mx(
+                out=q_codes[:, part * BANK : (part + 1) * BANK].bitcast(FP8X4),
+                scales=q_scales[:, part * BANK : (part + 1) * BANK],
+                in_=q_grouped_of[rnd][:],
+            )
+
+        def attend_scores(n):
+            it, h = n // HEADS, n % HEADS
+            q_codes, q_scales = q_mx_of[it]
+            scores = acc_psum.tile([P, COLS], F32, tag="acc")
+            for half in range(HALVES):
+                q_first = ((h // HEAD_GROUP) * HALVES + half) * BANK + (h % HEAD_GROUP) * P
+                k_first = (h * HALVES + half) * COLS
+                nc.tensor.matmul_mx(
+                    out=scores[:],
+                    lhsT=q_codes[:, q_first : q_first + P].bitcast(FP8X4),
+                    lhsT_scale=q_scales[:, q_first : q_first + P],
+                    rhs=k_codes[:, k_first : k_first + COLS].bitcast(FP8X4),
+                    rhs_scale=k_scales[:, k_first : k_first + COLS],
+                    start=(half == 0),
+                    stop=(half == HALVES - 1),
+                )
+            neg_max = soft.tile([P, 1], F32)
+            nc.vector.tensor_reduce(
+                out=neg_max[:], in_=scores[:], axis=mybir.AxisListType.X, op=ALU.max, negate=True
+            )
+            scores_of[n] = (scores, neg_max)
+
+        def attend_finish(n):
+            it, h = n // HEADS, n % HEADS
+            scores, neg_max = scores_of[n]
+            probs = soft.tile([P, COLS], F32)
+            total = soft.tile([P, 1], F32)
+            nc.scalar.activation(
+                out=probs[:], in_=scores[:], func=ACT.Exp, bias=neg_max[:, 0:1], scale=1.0,
+                accum_out=total[:, 0:1],
+            )
+            inverse = soft.tile([P, 1], F32)
+            nc.vector.reciprocal(out=inverse[:], in_=total[:])
+            nc.gpsimd.tensor_scalar(
+                out=probs[:], in0=probs[:], scalar1=inverse[:, 0:1], scalar2=0.0,
+                op0=ALU.mult, op1=ALU.add,
+            )
+            nc.sync.dma_start(out=out_view[:, h, it, :], in_=probs[:])
+
+        ident_f32 = keep.tile([P, P], F32)
+        make_identity(nc, ident_f32[:])
+        ident_bf16 = keep.tile([P, P], BF16)
+        make_identity(nc, ident_bf16[:])
+        w_codes = keep.tile([P, (2 * HEADS + 1) * HEAD_DIM], U32, align_bytes=64)
+        w_scales = keep.tile([P, (2 * HEADS + 1) * HEAD_DIM], U8, align_bytes=64)
+        bias = keep.tile([P, HEADS], F32)
+        k_codes = keep.tile([P, HEADS * HALVES * COLS], U32, align_bytes=64)
+        k_scales = keep.tile([P, HEADS * HALVES * COLS], U8, align_bytes=64)
+
+        load_x(0)
+        with tc.tile_pool(name="setup", bufs=1) as setup:
+            w_raw = setup.tile([P, PACK, WIDTH], BF16)
+            nc.sync.dma_start(
+                out=w_raw[:].rearrange("p (u e) c -> p u (e c)", u=2),
+                in_=Wq.rearrange("(u p e) c -> p u (e c)", u=2, e=2),
+            )
+            w_grouped = setup.tile([P, 2 * HEADS + 1, HEAD_DIM * PACK], BF16, align_bytes=64)
+            nc.vector.memset(w_grouped[:, 0 : 2 * HEADS + 1 : 2, :], 0.0)
+            bq_rows = setup.tile([P, P], BF16)
+            nc.vector.memset(bq_rows[:], 0.0)
+            for a in range(2):
+                nc.sync.dma_start(
+                    out=bq_rows[0:HEADS, a * HEAD_DIM : (a + 1) * HEAD_DIM],
+                    in_=bq.rearrange("(h d) -> h d", h=HEADS),
+                )
+            load_x(1)
+            load_keys(0)
+            load_keys(1)
+            load_keys(2)
+            turn_x(0)
+            nc.vector.tensor_copy(
+                out=w_grouped[:, 1 : 2 * HEADS : 2, :].rearrange("p h (d t) -> p h d t", t=PACK),
+                in_=w_raw[:].rearrange("p t (h d) -> p h d t", h=HEADS),
+            )
+            w_flat = w_grouped[:].rearrange("p b c -> p (b c)")
+            for first, words in ((0, 1024), (1024, HEAD_DIM)):
+                nc.vector.quantize_mx(
+                    out=w_codes[:, first : first + words].bitcast(FP8X4),
+                    scales=w_scales[:, first : first + words],
+                    in_=w_flat[:, first * PACK : (first + words) * PACK],
+                )
+            bq_turned = turn_psum.tile([P, P], BF16, tag="turn")
+            nc.tensor.transpose(bq_turned[:], bq_rows[:], ident_bf16[:])
+            nc.vector.tensor_scalar(
+                out=bias[:], in0=bq_turned[:, 0:HEADS], scalar1=SCALING, scalar2=None, op0=ALU.mult
+            )
+            quantise_x(0)
+            pair_keys(0)
+
+        q_work = ctx.enter_context(tc.tile_pool(name="q_work", bufs=3))
+        q_mx = ctx.enter_context(tc.tile_pool(name="q_mx", bufs=3))
+        soft = ctx.enter_context(tc.tile_pool(name="soft", bufs=6))
+
+        for rnd in range(ROUNDS + 1):
+            x_job = rnd // 2 + 1 if rnd % 2 == 0 else X_JOBS
+            if rnd + 3 < KEY_JOBS:
+                load_keys(rnd + 3)
+            if x_job + 1 < X_JOBS:
+                load_x(x_job + 1)
+            if x_job < X_JOBS:
+                turn_x(x_job)
+            if 1 <= rnd <= KEY_JOBS:
+                quantise_keys(rnd - 1)
+            if x_job < X_JOBS:
+                quantise_x(x_job)
+            if rnd + 1 < KEY_JOBS:
+                pair_keys(rnd + 1)
+            for h4 in range(HEAD_GROUP):
+                if rnd < ROUNDS:
+                    project_head(rnd, h4)
+                if rnd >= ATTEND_FROM:
+                    n = (rnd - ATTEND_FROM) * HEAD_GROUP + h4
+                    attend_scores(n)
+                    if n > 0:
+                        attend_finish(n - 1)
+            if rnd < ROUNDS:
+                quantise_q(rnd)
+            if rnd < KEY_JOBS:
+                turn_keys(rnd)
+        attend_finish(COL_TILES * HEADS - 1)

@@ -25,7 +25,10 @@ SCALING = 1.0 / 32.0
 X_JOBS = COL_TILES * HALVES
 KEY_JOBS = HALVES * COL_TILES
 ROUNDS = COL_TILES * (HEADS // HEAD_GROUP) * HALVES
-ATTEND_FROM = KEY_JOBS + 1
+JOB_BANKS = 4
+RUN = 2
+KEY_BANKS_ON_VECTOR = (0,)
+X_BANKS_ON_VECTOR = (0, 2)
 
 FLOPS = 2 * ROWS * COLS * WIDTH * WIDTH + 2 * HEADS * COLS * COLS * ROWS * HEAD_DIM
 
@@ -48,13 +51,13 @@ def tile_rowselfattention_pa_t_kernel(tc, x, Wq, bq, k, out):
         x_in = ctx.enter_context(tc.tile_pool(name="x_in", bufs=3))
         x_work = ctx.enter_context(tc.tile_pool(name="x_work", bufs=2))
         x_mx = ctx.enter_context(tc.tile_pool(name="x_mx", bufs=4))
-        turn_psum = ctx.enter_context(tc.psum_pool(name="turn_psum", bufs=2))
-        acc_psum = ctx.enter_context(tc.psum_pool(name="acc_psum", bufs=6))
+        turn_psum = ctx.enter_context(tc.psum_pool(name="turn_psum", bufs=4))
+        acc_psum = ctx.enter_context(tc.psum_pool(name="acc_psum", bufs=4))
 
         x_raw_of, x_grouped_of, x_mx_of = {}, {}, {}
         k_raw_of, k_pairs_of, k_grouped_of = {}, {}, {}
         q_grouped_of, q_mx_of = {}, {}
-        scores_of = {}
+        scores_of, probs_of = {}, {}
 
         def load_x(job):
             it, half = job // HALVES, job % HALVES
@@ -74,11 +77,19 @@ def tile_rowselfattention_pa_t_kernel(tc, x, Wq, bq, k, out):
             )
             k_raw_of[job] = k_raw
 
-        def turn_x(job):
+        def empty_bank(on_vector, dst, src):
+            if on_vector:
+                nc.vector.tensor_copy(out=dst, in_=src)
+            else:
+                nc.scalar.copy(out=dst, in_=src)
+
+        def turn_x(job, banks, vector_banks):
             x_words = x_raw_of[job][:].bitcast(F32)
-            x_grouped = x_work.tile([P, HALF_ROWS * P * PACK], BF16, align_bytes=64)
-            x_grouped_words = x_grouped[:].bitcast(F32)
-            for bank in range(HALF_ROWS // 2):
+            if banks[0] == 0:
+                x_grouped = x_work.tile([P, HALF_ROWS * P * PACK], BF16, align_bytes=64)
+                x_grouped_of[job] = x_grouped
+            x_grouped_words = x_grouped_of[job][:].bitcast(F32)
+            for bank in banks:
                 turned = turn_psum.tile([P, 2, 2, P], F32, tag="turn")
                 for s2 in range(2):
                     slot = 2 * bank + s2
@@ -88,15 +99,13 @@ def tile_rowselfattention_pa_t_kernel(tc, x, Wq, bq, k, out):
                         nc.tensor.transpose(
                             turned[:, s2, u, :], x_words[:, first : first + P], ident_f32[:]
                         )
-                dst = x_grouped_words[:, bank * BANK : (bank + 1) * BANK].rearrange(
-                    "p (s i u) -> p s i u", s=2, u=2
+                empty_bank(
+                    bank in vector_banks,
+                    x_grouped_words[:, bank * BANK : (bank + 1) * BANK].rearrange(
+                        "p (s i u) -> p s i u", s=2, u=2
+                    ),
+                    turned[:].rearrange("p s u i -> p s i u"),
                 )
-                src = turned[:].rearrange("p s u i -> p s i u")
-                if bank % 2 == 0:
-                    nc.vector.tensor_copy(out=dst, in_=src)
-                else:
-                    nc.scalar.copy(out=dst, in_=src)
-            x_grouped_of[job] = x_grouped
 
         def quantise_x(job):
             x_codes = x_mx.tile([P, HALF_ROWS * P], U32, align_bytes=64)
@@ -106,25 +115,26 @@ def tile_rowselfattention_pa_t_kernel(tc, x, Wq, bq, k, out):
             )
             x_mx_of[job] = (x_codes, x_scales)
 
-        def pair_keys(job):
-            k_raw = k_raw_of[job]
-            k_pairs = k_work.tile([P, HALF_ROWS * WIDTH], BF16)
-            for u in range(2):
-                nc.vector.tensor_copy(
-                    out=k_pairs[:, u * 2048 : (u + 1) * 2048].rearrange(
-                        "p (h a d e) -> p h a d e", h=HEADS, a=2, e=2
-                    ),
-                    in_=k_raw[:, u * 2048 : (u + 1) * 2048].rearrange(
-                        "p (a e h d) -> p h a d e", a=2, e=2, h=HEADS
-                    ),
-                )
-            k_pairs_of[job] = k_pairs
+        def pair_keys(job, u):
+            if u == 0:
+                k_pairs = k_work.tile([P, HALF_ROWS * WIDTH], BF16)
+                k_pairs_of[job] = k_pairs
+            nc.vector.tensor_copy(
+                out=k_pairs_of[job][:, u * 2048 : (u + 1) * 2048].rearrange(
+                    "p (h a d e) -> p h a d e", h=HEADS, a=2, e=2
+                ),
+                in_=k_raw_of[job][:, u * 2048 : (u + 1) * 2048].rearrange(
+                    "p (a e h d) -> p h a d e", a=2, e=2, h=HEADS
+                ),
+            )
 
-        def turn_keys(job):
+        def turn_keys(job, banks, vector_banks):
             k_words = k_pairs_of[job][:].bitcast(F32)
-            k_grouped = k_work.tile([P, HEADS * P * PACK], BF16, align_bytes=64)
-            k_grouped_words = k_grouped[:].bitcast(F32)
-            for bank in range(HEADS // 2):
+            if banks[0] == 0:
+                k_grouped = k_work.tile([P, HEADS * P * PACK], BF16, align_bytes=64)
+                k_grouped_of[job] = k_grouped
+            k_grouped_words = k_grouped_of[job][:].bitcast(F32)
+            for bank in banks:
                 turned = turn_psum.tile([P, 2, 2, P], F32, tag="turn")
                 for h2 in range(2):
                     for u in range(2):
@@ -132,13 +142,13 @@ def tile_rowselfattention_pa_t_kernel(tc, x, Wq, bq, k, out):
                         nc.tensor.transpose(
                             turned[:, h2, u, :], k_words[:, first : first + P], ident_f32[:]
                         )
-                nc.scalar.copy(
-                    out=k_grouped_words[:, bank * BANK : (bank + 1) * BANK].rearrange(
+                empty_bank(
+                    bank in vector_banks,
+                    k_grouped_words[:, bank * BANK : (bank + 1) * BANK].rearrange(
                         "p (h j u) -> p h j u", h=2, u=2
                     ),
-                    in_=turned[:].rearrange("p h u j -> p h j u"),
+                    turned[:].rearrange("p h u j -> p h j u"),
                 )
-            k_grouped_of[job] = k_grouped
 
         def quantise_keys(job):
             half, jt = job // COL_TILES, job % COL_TILES
@@ -214,8 +224,7 @@ def tile_rowselfattention_pa_t_kernel(tc, x, Wq, bq, k, out):
             )
             scores_of[n] = (scores, neg_max)
 
-        def attend_finish(n):
-            it, h = n // HEADS, n % HEADS
+        def attend_exp(n):
             scores, neg_max = scores_of[n]
             probs = soft.tile([P, COLS], F32)
             total = soft.tile([P, 1], F32)
@@ -223,6 +232,11 @@ def tile_rowselfattention_pa_t_kernel(tc, x, Wq, bq, k, out):
                 out=probs[:], in_=scores[:], func=ACT.Exp, bias=neg_max[:, 0:1], scale=1.0,
                 accum_out=total[:, 0:1],
             )
+            probs_of[n] = (probs, total)
+
+        def attend_store(n):
+            it, h = n // HEADS, n % HEADS
+            probs, total = probs_of[n]
             inverse = soft.tile([P, 1], F32)
             nc.vector.reciprocal(out=inverse[:], in_=total[:])
             nc.gpsimd.tensor_scalar(
@@ -260,8 +274,8 @@ def tile_rowselfattention_pa_t_kernel(tc, x, Wq, bq, k, out):
             load_x(1)
             load_keys(0)
             load_keys(1)
-            load_keys(2)
-            turn_x(0)
+            load_x(2)
+            turn_x(0, range(JOB_BANKS), ())
             nc.vector.tensor_copy(
                 out=w_grouped[:, 1 : 2 * HEADS : 2, :].rearrange("p h (d t) -> p h d t", t=PACK),
                 in_=w_raw[:].rearrange("p t (h d) -> p h d t", h=HEADS),
@@ -278,37 +292,47 @@ def tile_rowselfattention_pa_t_kernel(tc, x, Wq, bq, k, out):
             nc.vector.tensor_scalar(
                 out=bias[:], in0=bq_turned[:, 0:HEADS], scalar1=SCALING, scalar2=None, op0=ALU.mult
             )
+            turn_x(1, range(JOB_BANKS), ())
             quantise_x(0)
-            pair_keys(0)
+            pair_keys(0, 0)
+            pair_keys(0, 1)
+            quantise_x(1)
 
         q_work = ctx.enter_context(tc.tile_pool(name="q_work", bufs=3))
-        q_mx = ctx.enter_context(tc.tile_pool(name="q_mx", bufs=3))
-        soft = ctx.enter_context(tc.tile_pool(name="soft", bufs=6))
+        q_mx = ctx.enter_context(tc.tile_pool(name="q_mx", bufs=COL_TILES))
+        soft = ctx.enter_context(tc.tile_pool(name="soft", bufs=8))
 
-        for rnd in range(ROUNDS + 1):
-            x_job = rnd // 2 + 1 if rnd % 2 == 0 else X_JOBS
-            if rnd + 3 < KEY_JOBS:
-                load_keys(rnd + 3)
-            if x_job + 1 < X_JOBS:
-                load_x(x_job + 1)
-            if x_job < X_JOBS:
-                turn_x(x_job)
-            if 1 <= rnd <= KEY_JOBS:
-                quantise_keys(rnd - 1)
-            if x_job < X_JOBS:
-                quantise_x(x_job)
-            if rnd + 1 < KEY_JOBS:
-                pair_keys(rnd + 1)
-            for h4 in range(HEAD_GROUP):
-                if rnd < ROUNDS:
+        for rnd in range(ROUNDS):
+            step = rnd // 2
+            if rnd % 2 == 0:
+                if step + 2 < KEY_JOBS:
+                    load_keys(step + 2)
+                if step + 1 < KEY_JOBS:
+                    pair_keys(step + 1, 0)
+            else:
+                if step + 3 < X_JOBS:
+                    load_x(step + 3)
+                if step + 1 < KEY_JOBS:
+                    pair_keys(step + 1, 1)
+            for first in range(0, JOB_BANKS, RUN):
+                for h4 in range(first, first + RUN):
                     project_head(rnd, h4)
-                if rnd >= ATTEND_FROM:
-                    n = (rnd - ATTEND_FROM) * HEAD_GROUP + h4
-                    attend_scores(n)
-                    if n > 0:
-                        attend_finish(n - 1)
-            if rnd < ROUNDS:
-                quantise_q(rnd)
-            if rnd < KEY_JOBS:
-                turn_keys(rnd)
-        attend_finish(COL_TILES * HEADS - 1)
+                banks = range(first, first + RUN)
+                if rnd % 2 == 0:
+                    turn_keys(step, banks, KEY_BANKS_ON_VECTOR)
+                elif step + 2 < X_JOBS:
+                    turn_x(step + 2, banks, X_BANKS_ON_VECTOR)
+            quantise_q(rnd)
+            if rnd % 2 == 0:
+                quantise_keys(step)
+            elif step + 2 < X_JOBS:
+                quantise_x(step + 2)
+
+        maps = COL_TILES * HEADS
+        for n in range(maps + 2):
+            if n < maps:
+                attend_scores(n)
+            if 1 <= n <= maps:
+                attend_exp(n - 1)
+            if n >= 2:
+                attend_store(n - 2)

@@ -119,14 +119,14 @@ def tile_rowselfattention_pa_t_kernel(tc, x, Wq, bq, k, out):
             if u == 0:
                 k_pairs = k_work.tile([P, HALF_ROWS * WIDTH], BF16)
                 k_pairs_of[job] = k_pairs
-            nc.vector.tensor_copy(
-                out=k_pairs_of[job][:, u * 2048 : (u + 1) * 2048].rearrange(
-                    "p (h a d e) -> p h a d e", h=HEADS, a=2, e=2
-                ),
-                in_=k_raw_of[job][:, u * 2048 : (u + 1) * 2048].rearrange(
-                    "p (a e h d) -> p h a d e", a=2, e=2, h=HEADS
-                ),
+            pairs = k_pairs_of[job][:, u * 2048 : (u + 1) * 2048].rearrange(
+                "p (h a c i e) -> p a h c e i", h=HEADS, a=2, i=4, e=2
             )
+            rows = k_raw_of[job][:, u * 2048 : (u + 1) * 2048].rearrange(
+                "p (a e h c i) -> p a h c e i", a=2, e=2, h=HEADS, i=4
+            )
+            for a in range(2):
+                nc.vector.tensor_copy(out=pairs[:, a], in_=rows[:, a])
 
         def turn_keys(job, banks, vector_banks):
             k_words = k_pairs_of[job][:].bitcast(F32)
@@ -249,6 +249,10 @@ def tile_rowselfattention_pa_t_kernel(tc, x, Wq, bq, k, out):
         make_identity(nc, ident_f32[:])
         ident_bf16 = keep.tile([P, P], BF16)
         make_identity(nc, ident_bf16[:])
+        exp_in = keep.tile([P, 1], F32)
+        nc.vector.memset(exp_in[:], 0.0)
+        exp_out = keep.tile([P, 1], F32)
+        nc.scalar.activation(out=exp_out[:], in_=exp_in[:], func=ACT.Exp)
         w_codes = keep.tile([P, (2 * HEADS + 1) * HEAD_DIM], U32, align_bytes=64)
         w_scales = keep.tile([P, (2 * HEADS + 1) * HEAD_DIM], U8, align_bytes=64)
         bias = keep.tile([P, HEADS], F32)

@@ -26,7 +26,7 @@ X_JOBS = COL_TILES * HALVES
 KEY_JOBS = HALVES * COL_TILES
 ROUNDS = COL_TILES * (HEADS // HEAD_GROUP) * HALVES
 JOB_BANKS = 4
-RUN = 2
+RUN = 4
 KEY_BANKS_ON_VECTOR = (0,)
 X_BANKS_ON_VECTOR = (0, 2)
 
@@ -119,14 +119,14 @@ def tile_rowselfattention_pa_t_kernel(tc, x, Wq, bq, k, out):
             if u == 0:
                 k_pairs = k_work.tile([P, HALF_ROWS * WIDTH], BF16)
                 k_pairs_of[job] = k_pairs
-            pairs = k_pairs_of[job][:, u * 2048 : (u + 1) * 2048].rearrange(
-                "p (h a c i e) -> p a h c e i", h=HEADS, a=2, i=4, e=2
+            nc.vector.tensor_copy(
+                out=k_pairs_of[job][:, u * 2048 : (u + 1) * 2048].rearrange(
+                    "p (h a d e) -> p h a d e", h=HEADS, a=2, e=2
+                ),
+                in_=k_raw_of[job][:, u * 2048 : (u + 1) * 2048].rearrange(
+                    "p (a e h d) -> p h a d e", a=2, e=2, h=HEADS
+                ),
             )
-            rows = k_raw_of[job][:, u * 2048 : (u + 1) * 2048].rearrange(
-                "p (a e h c i) -> p a h c e i", a=2, e=2, h=HEADS, i=4
-            )
-            for a in range(2):
-                nc.vector.tensor_copy(out=pairs[:, a], in_=rows[:, a])
 
         def turn_keys(job, banks, vector_banks):
             k_words = k_pairs_of[job][:].bitcast(F32)
@@ -249,10 +249,6 @@ def tile_rowselfattention_pa_t_kernel(tc, x, Wq, bq, k, out):
         make_identity(nc, ident_f32[:])
         ident_bf16 = keep.tile([P, P], BF16)
         make_identity(nc, ident_bf16[:])
-        exp_in = keep.tile([P, 1], F32)
-        nc.vector.memset(exp_in[:], 0.0)
-        exp_out = keep.tile([P, 1], F32)
-        nc.scalar.activation(out=exp_out[:], in_=exp_in[:], func=ACT.Exp)
         w_codes = keep.tile([P, (2 * HEADS + 1) * HEAD_DIM], U32, align_bytes=64)
         w_scales = keep.tile([P, (2 * HEADS + 1) * HEAD_DIM], U8, align_bytes=64)
         bias = keep.tile([P, HEADS], F32)

@@ -19,14 +19,15 @@ ROWS, COLS, WIDTH, HEADS, HEAD_DIM = 16, 512, 512, 8, 64
 COL_TILES = COLS // P
 HALF_ROWS = 8
 HALVES = ROWS // HALF_ROWS
-HEAD_GROUP = 4
+PAIRS = HEADS // 2
 SCALING = 1.0 / 32.0
 
 X_JOBS = COL_TILES * HALVES
 KEY_JOBS = HALVES * COL_TILES
-ROUNDS = COL_TILES * (HEADS // HEAD_GROUP) * HALVES
+ROUNDS = X_JOBS * 2
+SIDE = BANK + BANK // 4
+STAGES = 3
 JOB_BANKS = 4
-RUN = 4
 KEY_BANKS_ON_VECTOR = (0,)
 X_BANKS_ON_VECTOR = (0, 2)
 
@@ -50,13 +51,13 @@ def tile_rowselfattention_pa_t_kernel(tc, x, Wq, bq, k, out):
         k_work = ctx.enter_context(tc.tile_pool(name="k_work", bufs=2))
         x_in = ctx.enter_context(tc.tile_pool(name="x_in", bufs=3))
         x_work = ctx.enter_context(tc.tile_pool(name="x_work", bufs=2))
-        x_mx = ctx.enter_context(tc.tile_pool(name="x_mx", bufs=4))
+        x_mx = ctx.enter_context(tc.tile_pool(name="x_mx", bufs=3))
         turn_psum = ctx.enter_context(tc.psum_pool(name="turn_psum", bufs=4))
         acc_psum = ctx.enter_context(tc.psum_pool(name="acc_psum", bufs=4))
 
         x_raw_of, x_grouped_of, x_mx_of = {}, {}, {}
         k_raw_of, k_pairs_of, k_grouped_of = {}, {}, {}
-        q_grouped_of, q_mx_of = {}, {}
+        q_grouped_of = {}
         scores_of, probs_of = {}, {}
 
         def load_x(job):
@@ -160,59 +161,66 @@ def tile_rowselfattention_pa_t_kernel(tc, x, Wq, bq, k, out):
                     in_=k_grouped_of[job][:, h * P * PACK : (h + 1) * P * PACK],
                 )
 
-        def project_head(rnd, h4):
-            it, group, half = rnd // 4, (rnd % 4) // 2, rnd % 2
-            h = group * HEAD_GROUP + h4
-            x_codes, x_scales = x_mx_of[it * HALVES + half]
-            if h4 == 0:
-                q_grouped = q_work.tile([P, HEAD_GROUP * P * PACK], BF16, align_bytes=64)
+        def project_pair(rnd, pair):
+            job, a = rnd // 2, rnd % 2
+            x_codes, x_scales = x_mx_of[job]
+            if pair == 0:
+                q_grouped = q_work.tile([P, PAIRS * P * PACK], BF16, align_bytes=64)
                 q_grouped_of[rnd] = q_grouped
             q_acc = acc_psum.tile([P, BANK], F32, tag="acc")
-            for a in range(2):
-                w_first = (2 * h + 1 - a) * HEAD_DIM
-                nc.tensor.matmul_mx(
-                    out=q_acc[:],
-                    lhsT=w_codes[:, w_first : w_first + P].bitcast(FP8X4),
-                    lhsT_scale=w_scales[:, w_first : w_first + P],
-                    rhs=x_codes[:, a * BANK : (a + 1) * BANK].bitcast(FP8X4),
-                    rhs_scale=x_scales[:, a * BANK : (a + 1) * BANK],
-                    start=(a == 0),
-                    stop=(a == 1),
-                )
+            nc.tensor.matmul_mx(
+                out=q_acc[:],
+                lhsT=w_codes[:, pair * P : (pair + 1) * P].bitcast(FP8X4),
+                lhsT_scale=w_scales[:, pair * P : (pair + 1) * P],
+                rhs=x_codes[:, a * BANK : (a + 1) * BANK].bitcast(FP8X4),
+                rhs_scale=x_scales[:, a * BANK : (a + 1) * BANK],
+                start=True,
+                stop=True,
+            )
             nc.scalar.activation(
-                out=q_grouped_of[rnd][:, h4 * BANK : (h4 + 1) * BANK].rearrange(
+                out=q_grouped_of[rnd][:, pair * BANK : (pair + 1) * BANK].rearrange(
                     "p (i t) -> p i t", t=PACK
                 ),
                 in_=q_acc[:].rearrange("p (t i) -> p i t", t=PACK),
                 func=ACT.Identity,
-                bias=bias[:, h : h + 1],
+                bias=bias[:, pair : pair + 1],
                 scale=SCALING,
             )
 
+        def side(job, odd):
+            first = (2 * job + odd) * SIDE
+            return q_packed[:, first : first + SIDE]
+
         def quantise_q(rnd):
-            it, part = rnd // 4, rnd % 4
-            if part == 0:
-                q_codes = q_mx.tile([P, HALVES * HEADS * P], U32, align_bytes=64)
-                q_scales = q_mx.tile([P, HALVES * HEADS * P], U8, align_bytes=64)
-                q_mx_of[it] = (q_codes, q_scales)
-            q_codes, q_scales = q_mx_of[it]
+            job, a = rnd // 2, rnd % 2
+            packed = stages[job % STAGES][:] if a else side(job, 0)
             nc.vector.quantize_mx(
-                out=q_codes[:, part * BANK : (part + 1) * BANK].bitcast(FP8X4),
-                scales=q_scales[:, part * BANK : (part + 1) * BANK],
+                out=packed[:, 0:BANK].bitcast(FP8X4),
+                scales=packed[:, BANK:SIDE].bitcast(U8),
                 in_=q_grouped_of[rnd][:],
             )
 
+        def regroup(rnd):
+            job, a = rnd // 2, rnd % 2
+            even, odd, stage = side(job, 0), side(job, 1), stages[job % STAGES]
+            half_p = HEAD_DIM
+            if a == 0:
+                nc.sync.dma_start(out=odd[0:half_p, :], in_=even[half_p:P, :])
+            else:
+                nc.sync.dma_start(out=even[half_p:P, :], in_=stage[0:half_p, :])
+                nc.sync.dma_start(out=odd[half_p:P, :], in_=stage[half_p:P, :])
+
         def attend_scores(n):
             it, h = n // HEADS, n % HEADS
-            q_codes, q_scales = q_mx_of[it]
             scores = acc_psum.tile([P, COLS], F32, tag="acc")
             for half in range(HALVES):
-                q_first = ((h // HEAD_GROUP) * HALVES + half) * BANK + (h % HEAD_GROUP) * P
+                packed = side(it * HALVES + half, h % 2)
+                q_first = (h // 2) * P
                 k_first = (h * HALVES + half) * COLS
                 nc.tensor.matmul_mx(
                     out=scores[:],
-                    lhsT=q_codes[:, q_first : q_first + P].bitcast(FP8X4),
-                    lhsT_scale=q_scales[:, q_first : q_first + P],
+                    lhsT=packed[:, q_first : q_first + P].bitcast(FP8X4),
+                    lhsT_scale=packed[:, BANK:SIDE].bitcast(U8)[:, q_first : q_first + P],
                     rhs=k_codes[:, k_first : k_first + COLS].bitcast(FP8X4),
                     rhs_scale=k_scales[:, k_first : k_first + COLS],
                     start=(half == 0),
@@ -249,11 +257,20 @@ def tile_rowselfattention_pa_t_kernel(tc, x, Wq, bq, k, out):
         make_identity(nc, ident_f32[:])
         ident_bf16 = keep.tile([P, P], BF16)
         make_identity(nc, ident_bf16[:])
-        w_codes = keep.tile([P, (2 * HEADS + 1) * HEAD_DIM], U32, align_bytes=64)
-        w_scales = keep.tile([P, (2 * HEADS + 1) * HEAD_DIM], U8, align_bytes=64)
-        bias = keep.tile([P, HEADS], F32)
+        w_codes = keep.tile([P, WIDTH], U32, align_bytes=64)
+        w_scales = keep.tile([P, WIDTH], U8, align_bytes=64)
+        bias = keep.tile([P, PAIRS], F32)
         k_codes = keep.tile([P, HEADS * HALVES * COLS], U32, align_bytes=64)
         k_scales = keep.tile([P, HEADS * HALVES * COLS], U8, align_bytes=64)
+        q_packed = keep.tile([P, X_JOBS * 2 * SIDE], I32, align_bytes=64)
+        nc.gpsimd.memset(
+            q_packed[:].rearrange("p (n w) -> p n w", w=SIDE)[:, :, BANK:SIDE], 0
+        )
+        stages = []
+        for i in range(STAGES):
+            stage_tile = keep.tile([P, SIDE], I32, align_bytes=64, name="stage%d" % i)
+            nc.gpsimd.memset(stage_tile[:, BANK:SIDE], 0)
+            stages.append(stage_tile)
 
         load_x(0)
         with tc.tile_pool(name="setup", bufs=1) as setup:
@@ -262,35 +279,26 @@ def tile_rowselfattention_pa_t_kernel(tc, x, Wq, bq, k, out):
                 out=w_raw[:].rearrange("p (u e) c -> p u (e c)", u=2),
                 in_=Wq.rearrange("(u p e) c -> p u (e c)", u=2, e=2),
             )
-            w_grouped = setup.tile([P, 2 * HEADS + 1, HEAD_DIM * PACK], BF16, align_bytes=64)
-            nc.vector.memset(w_grouped[:, 0 : 2 * HEADS + 1 : 2, :], 0.0)
+            w_grouped = setup.tile([P, WIDTH * PACK], BF16, align_bytes=64)
             bq_rows = setup.tile([P, P], BF16)
             nc.vector.memset(bq_rows[:], 0.0)
-            for a in range(2):
-                nc.sync.dma_start(
-                    out=bq_rows[0:HEADS, a * HEAD_DIM : (a + 1) * HEAD_DIM],
-                    in_=bq.rearrange("(h d) -> h d", h=HEADS),
-                )
+            nc.sync.dma_start(out=bq_rows[0:PAIRS, :], in_=bq.rearrange("(h d) -> h d", h=PAIRS))
             load_x(1)
             load_keys(0)
             load_keys(1)
             load_x(2)
             turn_x(0, range(JOB_BANKS), ())
             nc.vector.tensor_copy(
-                out=w_grouped[:, 1 : 2 * HEADS : 2, :].rearrange("p h (d t) -> p h d t", t=PACK),
-                in_=w_raw[:].rearrange("p t (h d) -> p h d t", h=HEADS),
+                out=w_grouped[:].rearrange("p (c t) -> p c t", t=PACK),
+                in_=w_raw[:].rearrange("p t c -> p c t"),
             )
-            w_flat = w_grouped[:].rearrange("p b c -> p (b c)")
-            for first, words in ((0, 1024), (1024, HEAD_DIM)):
-                nc.vector.quantize_mx(
-                    out=w_codes[:, first : first + words].bitcast(FP8X4),
-                    scales=w_scales[:, first : first + words],
-                    in_=w_flat[:, first * PACK : (first + words) * PACK],
-                )
+            nc.vector.quantize_mx(
+                out=w_codes[:].bitcast(FP8X4), scales=w_scales[:], in_=w_grouped[:]
+            )
             bq_turned = turn_psum.tile([P, P], BF16, tag="turn")
             nc.tensor.transpose(bq_turned[:], bq_rows[:], ident_bf16[:])
             nc.vector.tensor_scalar(
-                out=bias[:], in0=bq_turned[:, 0:HEADS], scalar1=SCALING, scalar2=None, op0=ALU.mult
+                out=bias[:], in0=bq_turned[:, 0:PAIRS], scalar1=SCALING, scalar2=None, op0=ALU.mult
             )
             turn_x(1, range(JOB_BANKS), ())
             quantise_x(0)
@@ -299,7 +307,6 @@ def tile_rowselfattention_pa_t_kernel(tc, x, Wq, bq, k, out):
             quantise_x(1)
 
         q_work = ctx.enter_context(tc.tile_pool(name="q_work", bufs=3))
-        q_mx = ctx.enter_context(tc.tile_pool(name="q_mx", bufs=COL_TILES))
         soft = ctx.enter_context(tc.tile_pool(name="soft", bufs=8))
 
         for rnd in range(ROUNDS):
@@ -314,19 +321,24 @@ def tile_rowselfattention_pa_t_kernel(tc, x, Wq, bq, k, out):
                     load_x(step + 3)
                 if step + 1 < KEY_JOBS:
                     pair_keys(step + 1, 1)
-            for first in range(0, JOB_BANKS, RUN):
-                for h4 in range(first, first + RUN):
-                    project_head(rnd, h4)
-                banks = range(first, first + RUN)
-                if rnd % 2 == 0:
-                    turn_keys(step, banks, KEY_BANKS_ON_VECTOR)
-                elif step + 2 < X_JOBS:
-                    turn_x(step + 2, banks, X_BANKS_ON_VECTOR)
-            quantise_q(rnd)
+            if rnd >= 1:
+                quantise_q(rnd - 1)
+            for pair in range(PAIRS):
+                project_pair(rnd, pair)
+            banks = range(JOB_BANKS)
             if rnd % 2 == 0:
+                turn_keys(step, banks, KEY_BANKS_ON_VECTOR)
+                if 1 <= step and step + 1 < X_JOBS:
+                    quantise_x(step + 1)
+            else:
+                if step + 2 < X_JOBS:
+                    turn_x(step + 2, banks, X_BANKS_ON_VECTOR)
                 quantise_keys(step)
-            elif step + 2 < X_JOBS:
-                quantise_x(step + 2)
+            if rnd >= 1:
+                regroup(rnd - 1)
+
+        quantise_q(ROUNDS - 1)
+        regroup(ROUNDS - 1)
 
         maps = COL_TILES * HEADS
         for n in range(maps + 2):

@@ -18,6 +18,7 @@ BANK = 512
 ROWS, COLS, WIDTH, HEADS, HEAD_DIM = 16, 512, 512, 8, 64
 COL_TILES = COLS // P
 HALF_ROWS = 8
+GROUP_ROWS = 4
 HALVES = ROWS // HALF_ROWS
 PAIRS = HEADS // 2
 SCALING = 1.0 / 32.0
@@ -25,17 +26,12 @@ SCALING = 1.0 / 32.0
 X_JOBS = COL_TILES * HALVES
 KEY_JOBS = HALVES * COL_TILES
 ROUNDS = X_JOBS * 2
-SIDE = BANK + BANK // 4
-STAGES = 3
 JOB_BANKS = 4
-KEY_BANKS_ON_VECTOR = (0,)
-X_BANKS_ON_VECTOR = (0, 2)
+SIDE = BANK + BANK // 4
+VECTOR_BANKS = (0,)
+LOADS_DONE = 10
 
 FLOPS = 2 * ROWS * COLS * WIDTH * WIDTH + 2 * HEADS * COLS * COLS * ROWS * HEAD_DIM
-
-
-def row_in_half(a, t):
-    return 4 * (t // 2) + 2 * a + (t % 2)
 
 
 def tile_rowselfattention_pa_t_kernel(tc, x, Wq, bq, k, out):
@@ -47,174 +43,278 @@ def tile_rowselfattention_pa_t_kernel(tc, x, Wq, bq, k, out):
     with ExitStack() as ctx:
         ctx.enter_context(tc.manual_schedule())
         keep = ctx.enter_context(tc.tile_pool(name="keep", bufs=1))
-        k_in = ctx.enter_context(tc.tile_pool(name="k_in", bufs=3))
-        k_work = ctx.enter_context(tc.tile_pool(name="k_work", bufs=2))
-        x_in = ctx.enter_context(tc.tile_pool(name="x_in", bufs=3))
-        x_work = ctx.enter_context(tc.tile_pool(name="x_work", bufs=2))
-        x_mx = ctx.enter_context(tc.tile_pool(name="x_mx", bufs=3))
         turn_psum = ctx.enter_context(tc.psum_pool(name="turn_psum", bufs=4))
         acc_psum = ctx.enter_context(tc.psum_pool(name="acc_psum", bufs=4))
 
-        x_raw_of, x_grouped_of, x_mx_of = {}, {}, {}
-        k_raw_of, k_pairs_of, k_grouped_of = {}, {}, {}
-        q_grouped_of = {}
-        scores_of, probs_of = {}, {}
+        ident_f32 = keep.tile([P, P], F32)
+        w_codes = keep.tile([P, WIDTH], U32, align_bytes=64)
+        w_scales = keep.tile([P, WIDTH], U8, align_bytes=64)
+        bias = keep.tile([P, PAIRS], F32)
+        k_codes = keep.tile([P, HEADS * HALVES * COLS], U32, align_bytes=64)
+        k_scales = keep.tile([P, HEADS * HALVES * COLS], U8, align_bytes=64)
+        q_packed = keep.tile([P, X_JOBS * 3 * SIDE], I32, align_bytes=64)
 
-        def load_x(job):
-            it, half = job // HALVES, job % HALVES
-            x_raw = x_in.tile([P, HALF_ROWS * WIDTH], BF16)
-            nc.sync.dma_start(
-                out=x_raw[:].rearrange("p (r e) -> p r e", r=HALF_ROWS),
-                in_=x_view[:, it, half * HALF_ROWS : (half + 1) * HALF_ROWS, :],
-            )
-            x_raw_of[job] = x_raw
-
-        def load_keys(job):
-            half, jt = job // COL_TILES, job % COL_TILES
-            k_raw = k_in.tile([P, HALF_ROWS * WIDTH], BF16)
-            nc.sync.dma_start(
-                out=k_raw[:].rearrange("p (r e) -> p r e", r=HALF_ROWS),
-                in_=k_view[:, jt, half * HALF_ROWS : (half + 1) * HALF_ROWS, :],
-            )
-            k_raw_of[job] = k_raw
-
-        def empty_bank(on_vector, dst, src):
-            if on_vector:
-                nc.vector.tensor_copy(out=dst, in_=src)
-            else:
-                nc.scalar.copy(out=dst, in_=src)
-
-        def turn_x(job, banks, vector_banks):
-            x_words = x_raw_of[job][:].bitcast(F32)
-            if banks[0] == 0:
-                x_grouped = x_work.tile([P, HALF_ROWS * P * PACK], BF16, align_bytes=64)
-                x_grouped_of[job] = x_grouped
-            x_grouped_words = x_grouped_of[job][:].bitcast(F32)
-            for bank in banks:
-                turned = turn_psum.tile([P, 2, 2, P], F32, tag="turn")
-                for s2 in range(2):
-                    slot = 2 * bank + s2
-                    row = row_in_half(slot // PACK, slot % PACK)
-                    for u in range(2):
-                        first = row * (WIDTH // 2) + u * P
-                        nc.tensor.transpose(
-                            turned[:, s2, u, :], x_words[:, first : first + P], ident_f32[:]
-                        )
-                empty_bank(
-                    bank in vector_banks,
-                    x_grouped_words[:, bank * BANK : (bank + 1) * BANK].rearrange(
-                        "p (s i u) -> p s i u", s=2, u=2
-                    ),
-                    turned[:].rearrange("p s u i -> p s i u"),
-                )
-
-        def quantise_x(job):
-            x_codes = x_mx.tile([P, HALF_ROWS * P], U32, align_bytes=64)
-            x_scales = x_mx.tile([P, HALF_ROWS * P], U8, align_bytes=64)
-            nc.vector.quantize_mx(
-                out=x_codes[:].bitcast(FP8X4), scales=x_scales[:], in_=x_grouped_of[job][:]
-            )
-            x_mx_of[job] = (x_codes, x_scales)
-
-        def pair_keys(job, u):
-            if u == 0:
-                k_pairs = k_work.tile([P, HALF_ROWS * WIDTH], BF16)
-                k_pairs_of[job] = k_pairs
-            nc.vector.tensor_copy(
-                out=k_pairs_of[job][:, u * 2048 : (u + 1) * 2048].rearrange(
-                    "p (h a d e) -> p h a d e", h=HEADS, a=2, e=2
-                ),
-                in_=k_raw_of[job][:, u * 2048 : (u + 1) * 2048].rearrange(
-                    "p (a e h d) -> p h a d e", a=2, e=2, h=HEADS
-                ),
-            )
-
-        def turn_keys(job, banks, vector_banks):
-            k_words = k_pairs_of[job][:].bitcast(F32)
-            if banks[0] == 0:
-                k_grouped = k_work.tile([P, HEADS * P * PACK], BF16, align_bytes=64)
-                k_grouped_of[job] = k_grouped
-            k_grouped_words = k_grouped_of[job][:].bitcast(F32)
-            for bank in banks:
-                turned = turn_psum.tile([P, 2, 2, P], F32, tag="turn")
-                for h2 in range(2):
-                    for u in range(2):
-                        first = (u * HEADS + 2 * bank + h2) * P
-                        nc.tensor.transpose(
-                            turned[:, h2, u, :], k_words[:, first : first + P], ident_f32[:]
-                        )
-                empty_bank(
-                    bank in vector_banks,
-                    k_grouped_words[:, bank * BANK : (bank + 1) * BANK].rearrange(
-                        "p (h j u) -> p h j u", h=2, u=2
-                    ),
-                    turned[:].rearrange("p h u j -> p h j u"),
-                )
-
-        def quantise_keys(job):
-            half, jt = job // COL_TILES, job % COL_TILES
-            for h in range(HEADS):
-                first = (h * HALVES + half) * COLS + jt * P
-                nc.vector.quantize_mx(
-                    out=k_codes[:, first : first + P].bitcast(FP8X4),
-                    scales=k_scales[:, first : first + P],
-                    in_=k_grouped_of[job][:, h * P * PACK : (h + 1) * P * PACK],
-                )
-
-        def project_pair(rnd, pair):
-            job, a = rnd // 2, rnd % 2
-            x_codes, x_scales = x_mx_of[job]
-            if pair == 0:
-                q_grouped = q_work.tile([P, PAIRS * P * PACK], BF16, align_bytes=64)
-                q_grouped_of[rnd] = q_grouped
-            q_acc = acc_psum.tile([P, BANK], F32, tag="acc")
-            nc.tensor.matmul_mx(
-                out=q_acc[:],
-                lhsT=w_codes[:, pair * P : (pair + 1) * P].bitcast(FP8X4),
-                lhsT_scale=w_scales[:, pair * P : (pair + 1) * P],
-                rhs=x_codes[:, a * BANK : (a + 1) * BANK].bitcast(FP8X4),
-                rhs_scale=x_scales[:, a * BANK : (a + 1) * BANK],
-                start=True,
-                stop=True,
-            )
-            nc.scalar.activation(
-                out=q_grouped_of[rnd][:, pair * BANK : (pair + 1) * BANK].rearrange(
-                    "p (i t) -> p i t", t=PACK
-                ),
-                in_=q_acc[:].rearrange("p (t i) -> p i t", t=PACK),
-                func=ACT.Identity,
-                bias=bias[:, pair : pair + 1],
-                scale=SCALING,
-            )
-
-        def side(job, odd):
-            first = (2 * job + odd) * SIDE
+        def packed_queries(job, part):
+            first = (3 * job + part) * SIDE
             return q_packed[:, first : first + SIDE]
 
-        def quantise_q(rnd):
-            job, a = rnd // 2, rnd % 2
-            packed = stages[job % STAGES][:] if a else side(job, 0)
-            nc.vector.quantize_mx(
-                out=packed[:, 0:BANK].bitcast(FP8X4),
-                scales=packed[:, BANK:SIDE].bitcast(U8),
-                in_=q_grouped_of[rnd][:],
-            )
+        with ExitStack() as first_phase:
+            k_in = first_phase.enter_context(tc.tile_pool(name="k_in", bufs=3))
+            x_in = first_phase.enter_context(tc.tile_pool(name="x_in", bufs=3))
+            k_work = first_phase.enter_context(tc.tile_pool(name="k_work", bufs=2))
+            x_work = first_phase.enter_context(tc.tile_pool(name="x_work", bufs=2))
+            x_mx = first_phase.enter_context(tc.tile_pool(name="x_mx", bufs=3))
+            q_work = first_phase.enter_context(tc.tile_pool(name="q_work", bufs=3))
+            x_raw_of, x_grouped_of, x_mx_of = {}, {}, {}
+            k_raw_of, k_pairs_of, k_grouped_of = {}, {}, {}
+            q_grouped_of = {}
 
-        def regroup(rnd):
-            job, a = rnd // 2, rnd % 2
-            even, odd, stage = side(job, 0), side(job, 1), stages[job % STAGES]
-            half_p = HEAD_DIM
-            if a == 0:
-                nc.sync.dma_start(out=odd[0:half_p, :], in_=even[half_p:P, :])
-            else:
-                nc.sync.dma_start(out=even[half_p:P, :], in_=stage[0:half_p, :])
-                nc.sync.dma_start(out=odd[half_p:P, :], in_=stage[half_p:P, :])
+            def load_x(job, groups):
+                it, half = job // HALVES, job % HALVES
+                if groups[0] == 0:
+                    x_raw = x_in.tile([P, HALF_ROWS * WIDTH], BF16)
+                    x_raw_of[job] = x_raw
+                first, count = GROUP_ROWS * groups[0], GROUP_ROWS * len(groups)
+                nc.sync.dma_start(
+                    out=x_raw_of[job][:, first * WIDTH : (first + count) * WIDTH].rearrange(
+                        "p (r e) -> p r e", r=count
+                    ),
+                    in_=x_view[:, it, half * HALF_ROWS + first : half * HALF_ROWS + first + count, :],
+                )
+
+            def load_keys(job, groups):
+                half, jt = job // COL_TILES, job % COL_TILES
+                if groups[0] == 0:
+                    k_raw = k_in.tile([P, HALF_ROWS * WIDTH], BF16)
+                    k_raw_of[job] = k_raw
+                first, count = GROUP_ROWS * groups[0], GROUP_ROWS * len(groups)
+                nc.sync.dma_start(
+                    out=k_raw_of[job][:, first * WIDTH : (first + count) * WIDTH].rearrange(
+                        "p (r e) -> p r e", r=count
+                    ),
+                    in_=k_view[:, jt, half * HALF_ROWS + first : half * HALF_ROWS + first + count, :],
+                )
+
+            def empty_bank(on_vector, dst, src):
+                if on_vector:
+                    nc.vector.tensor_copy(out=dst, in_=src)
+                else:
+                    nc.scalar.copy(out=dst, in_=src)
+
+            def turn_x(job, banks, vector_banks):
+                x_words = x_raw_of[job][:].bitcast(F32)
+                if banks[0] == 0:
+                    x_grouped = x_work.tile([P, HALF_ROWS * P * PACK], BF16, align_bytes=64)
+                    x_grouped_of[job] = x_grouped
+                x_grouped_words = x_grouped_of[job][:].bitcast(F32)
+                for bank in banks:
+                    turned = turn_psum.tile([P, 2, 2, P], F32, tag="turn")
+                    for r2 in range(2):
+                        for u in range(2):
+                            first = (2 * bank + r2) * (WIDTH // 2) + u * P
+                            nc.tensor.transpose(
+                                turned[:, r2, u, :], x_words[:, first : first + P], ident_f32[:]
+                            )
+                    empty_bank(
+                        bank in vector_banks,
+                        x_grouped_words[:, bank * BANK : (bank + 1) * BANK].rearrange(
+                            "p (s i u) -> p s i u", s=2, u=2
+                        ),
+                        turned[:].rearrange("p s u i -> p s i u"),
+                    )
+
+            def quantise_x(job, groups):
+                if groups[0] == 0:
+                    x_codes = x_mx.tile([P, HALF_ROWS * P], U32, align_bytes=64)
+                    x_scales = x_mx.tile([P, HALF_ROWS * P], U8, align_bytes=64)
+                    x_mx_of[job] = (x_codes, x_scales)
+                x_codes, x_scales = x_mx_of[job]
+                first, last = BANK * groups[0], BANK * (groups[-1] + 1)
+                nc.vector.quantize_mx(
+                    out=x_codes[:, first:last].bitcast(FP8X4),
+                    scales=x_scales[:, first:last],
+                    in_=x_grouped_of[job][:, first * PACK : last * PACK],
+                )
+
+            def pair_keys(job, a):
+                if a == 0:
+                    k_pairs = k_work.tile([P, HALF_ROWS * WIDTH], BF16)
+                    k_pairs_of[job] = k_pairs
+                nc.vector.tensor_copy(
+                    out=k_pairs_of[job][:].rearrange(
+                        "p (u h a d e) -> p a u h d e", u=2, h=HEADS, a=2, e=2
+                    )[:, a],
+                    in_=k_raw_of[job][:, a * 2048 : (a + 1) * 2048].rearrange(
+                        "p (u e h d) -> p u h d e", u=2, e=2, h=HEADS
+                    ),
+                )
+
+            def turn_keys(job, vector_banks):
+                k_words = k_pairs_of[job][:].bitcast(F32)
+                k_grouped = k_work.tile([P, HEADS * P * PACK], BF16, align_bytes=64)
+                k_grouped_of[job] = k_grouped
+                k_grouped_words = k_grouped[:].bitcast(F32)
+                for bank in range(JOB_BANKS):
+                    turned = turn_psum.tile([P, 2, 2, P], F32, tag="turn")
+                    for h2 in range(2):
+                        for u in range(2):
+                            first = (u * HEADS + 2 * bank + h2) * P
+                            nc.tensor.transpose(
+                                turned[:, h2, u, :], k_words[:, first : first + P], ident_f32[:]
+                            )
+                    empty_bank(
+                        bank in vector_banks,
+                        k_grouped_words[:, bank * BANK : (bank + 1) * BANK].rearrange(
+                            "p (h j u) -> p h j u", h=2, u=2
+                        ),
+                        turned[:].rearrange("p h u j -> p h j u"),
+                    )
+
+            def quantise_keys(job):
+                half, jt = job // COL_TILES, job % COL_TILES
+                for h in range(HEADS):
+                    first = (h * HALVES + half) * COLS + jt * P
+                    nc.vector.quantize_mx(
+                        out=k_codes[:, first : first + P].bitcast(FP8X4),
+                        scales=k_scales[:, first : first + P],
+                        in_=k_grouped_of[job][:, h * P * PACK : (h + 1) * P * PACK],
+                    )
+
+            def project(rnd):
+                job, a = rnd // 2, rnd % 2
+                x_codes, x_scales = x_mx_of[job]
+                q_grouped = q_work.tile([P, PAIRS * P * PACK], BF16, align_bytes=64)
+                q_grouped_of[rnd] = q_grouped
+                for pair in range(PAIRS):
+                    q_acc = acc_psum.tile([P, BANK], F32, tag="acc")
+                    nc.tensor.matmul_mx(
+                        out=q_acc[:],
+                        lhsT=w_codes[:, pair * P : (pair + 1) * P].bitcast(FP8X4),
+                        lhsT_scale=w_scales[:, pair * P : (pair + 1) * P],
+                        rhs=x_codes[:, a * BANK : (a + 1) * BANK].bitcast(FP8X4),
+                        rhs_scale=x_scales[:, a * BANK : (a + 1) * BANK],
+                        start=True,
+                        stop=True,
+                    )
+                    nc.scalar.activation(
+                        out=q_grouped[:, pair * BANK : (pair + 1) * BANK].rearrange(
+                            "p (i t) -> p i t", t=PACK
+                        ),
+                        in_=q_acc[:].rearrange("p (t i) -> p i t", t=PACK),
+                        func=ACT.Identity,
+                        bias=bias[:, pair : pair + 1],
+                        scale=SCALING,
+                    )
+
+            def quantise_q(rnd):
+                job, a = rnd // 2, rnd % 2
+                packed = packed_queries(job, 2 * a)
+                nc.vector.quantize_mx(
+                    out=packed[:, 0:BANK].bitcast(FP8X4),
+                    scales=packed[:, BANK:SIDE].bitcast(U8),
+                    in_=q_grouped_of[rnd][:],
+                )
+
+            def regroup(job):
+                even, odd, both = (packed_queries(job, part) for part in range(3))
+                nc.sync.dma_start(out=odd[0:HEAD_DIM, :], in_=even[HEAD_DIM:P, :])
+                nc.sync.dma_start(out=odd[HEAD_DIM:P, :], in_=both[HEAD_DIM:P, :])
+                nc.sync.dma_start(out=even[HEAD_DIM:P, :], in_=both[0:HEAD_DIM, :])
+
+            with tc.tile_pool(name="setup", bufs=1) as setup:
+                w_raw = setup.tile([P, PACK, WIDTH], BF16)
+                nc.sync.dma_start(
+                    out=w_raw[:].rearrange("p (u e) c -> p u (e c)", u=2),
+                    in_=Wq.rearrange("(u p e) c -> p u (e c)", u=2, e=2),
+                )
+                load_x(0, (0,))
+                load_x(0, (1,))
+                bq_rows = setup.tile([P, P], BF16)
+                nc.vector.memset(bq_rows[:], 0.0)
+                nc.sync.dma_start(
+                    out=bq_rows[0:PAIRS, :], in_=bq.rearrange("(h d) -> h d", h=PAIRS)
+                )
+                load_keys(0, (0,))
+                load_keys(0, (1,))
+                load_x(1, (0, 1))
+                load_keys(1, (0, 1))
+                make_identity(nc, ident_f32[:])
+                ident_bf16 = setup.tile([P, P], BF16)
+                make_identity(nc, ident_bf16[:])
+                nc.gpsimd.memset(
+                    q_packed[:].rearrange("p (n w) -> p n w", w=SIDE)[:, :, BANK:SIDE], 0
+                )
+                w_grouped = setup.tile([P, WIDTH * PACK], BF16, align_bytes=64)
+                nc.vector.tensor_copy(
+                    out=w_grouped[:].rearrange("p (c t) -> p c t", t=PACK),
+                    in_=w_raw[:].rearrange("p t c -> p c t"),
+                )
+                nc.vector.quantize_mx(
+                    out=w_codes[:].bitcast(FP8X4), scales=w_scales[:], in_=w_grouped[:]
+                )
+                turn_x(0, (0, 1), (0,))
+                quantise_x(0, (0,))
+                bq_turned = acc_psum.tile([P, P], BF16, tag="acc")
+                nc.tensor.transpose(bq_turned[:], bq_rows[:], ident_bf16[:])
+                nc.vector.tensor_scalar(
+                    out=bias[:],
+                    in0=bq_turned[:, 0:PAIRS],
+                    scalar1=SCALING,
+                    scalar2=None,
+                    op0=ALU.mult,
+                )
+                turn_x(0, (2, 3), (2,))
+                quantise_x(0, (1,))
+                pair_keys(0, 0)
+
+            x_turn = {2 * job - 2: job for job in range(1, X_JOBS)}
+            k_turn = {2 * job + 1: job for job in range(KEY_JOBS - 1)}
+            k_turn[ROUNDS - 2] = KEY_JOBS - 1
+            moved = 0
+            for rnd in range(ROUNDS + 1):
+                if rnd % 2 == 0:
+                    if rnd == 0:
+                        project(rnd)
+                    if rnd // 2 < KEY_JOBS:
+                        pair_keys(rnd // 2, 1)
+                    if rnd in x_turn:
+                        turn_x(x_turn[rnd], range(JOB_BANKS), VECTOR_BANKS)
+                    if rnd in k_turn:
+                        turn_keys(k_turn[rnd], VECTOR_BANKS)
+                    if 0 < rnd < ROUNDS:
+                        project(rnd)
+                    if rnd >= 1:
+                        quantise_q(rnd - 1)
+                    if rnd - 1 in k_turn:
+                        quantise_keys(k_turn[rnd - 1])
+                else:
+                    project(rnd)
+                    if rnd - 1 in x_turn:
+                        quantise_x(x_turn[rnd - 1], (0, 1))
+                    if rnd // 2 + 1 < KEY_JOBS:
+                        pair_keys(rnd // 2 + 1, 0)
+                    quantise_q(rnd - 1)
+                    if rnd in k_turn:
+                        turn_keys(k_turn[rnd], VECTOR_BANKS)
+                    if rnd - 1 in k_turn:
+                        quantise_keys(k_turn[rnd - 1])
+                if rnd % 2 == 0 and rnd // 2 + 2 < X_JOBS:
+                    load_x(rnd // 2 + 2, (0, 1))
+                    load_keys(rnd // 2 + 2, (0, 1))
+                if rnd >= LOADS_DONE:
+                    while 2 * moved + 1 < rnd:
+                        regroup(moved)
+                        moved += 1
+
+        soft = ctx.enter_context(tc.tile_pool(name="soft", bufs=8))
+        probs_pool = ctx.enter_context(tc.tile_pool(name="probs_pool", bufs=16))
+        scores_of, probs_of, total_of = {}, {}, {}
 
         def attend_scores(n):
             it, h = n // HEADS, n % HEADS
             scores = acc_psum.tile([P, COLS], F32, tag="acc")
             for half in range(HALVES):
-                packed = side(it * HALVES + half, h % 2)
+                packed = packed_queries(it * HALVES + half, h % 2)
                 q_first = (h // 2) * P
                 k_first = (h * HALVES + half) * COLS
                 nc.tensor.matmul_mx(
@@ -234,117 +334,33 @@ def tile_rowselfattention_pa_t_kernel(tc, x, Wq, bq, k, out):
 
         def attend_exp(n):
             scores, neg_max = scores_of[n]
-            probs = soft.tile([P, COLS], F32)
-            total = soft.tile([P, 1], F32)
+            probs = probs_pool.tile([P, COLS], F32)
+            if n % 2 == 0:
+                total = soft.tile([P, 2], F32)
+                total_of[n // 2] = total
             nc.scalar.activation(
                 out=probs[:], in_=scores[:], func=ACT.Exp, bias=neg_max[:, 0:1], scale=1.0,
-                accum_out=total[:, 0:1],
+                accum_out=total_of[n // 2][:, n % 2 : n % 2 + 1],
             )
-            probs_of[n] = (probs, total)
+            probs_of[n] = probs
 
-        def attend_store(n):
-            it, h = n // HEADS, n % HEADS
-            probs, total = probs_of[n]
-            inverse = soft.tile([P, 1], F32)
-            nc.vector.reciprocal(out=inverse[:], in_=total[:])
-            nc.gpsimd.tensor_scalar(
-                out=probs[:], in0=probs[:], scalar1=inverse[:, 0:1], scalar2=0.0,
-                op0=ALU.mult, op1=ALU.add,
-            )
-            nc.sync.dma_start(out=out_view[:, h, it, :], in_=probs[:])
-
-        ident_f32 = keep.tile([P, P], F32)
-        make_identity(nc, ident_f32[:])
-        ident_bf16 = keep.tile([P, P], BF16)
-        make_identity(nc, ident_bf16[:])
-        w_codes = keep.tile([P, WIDTH], U32, align_bytes=64)
-        w_scales = keep.tile([P, WIDTH], U8, align_bytes=64)
-        bias = keep.tile([P, PAIRS], F32)
-        k_codes = keep.tile([P, HEADS * HALVES * COLS], U32, align_bytes=64)
-        k_scales = keep.tile([P, HEADS * HALVES * COLS], U8, align_bytes=64)
-        q_packed = keep.tile([P, X_JOBS * 2 * SIDE], I32, align_bytes=64)
-        nc.gpsimd.memset(
-            q_packed[:].rearrange("p (n w) -> p n w", w=SIDE)[:, :, BANK:SIDE], 0
-        )
-        stages = []
-        for i in range(STAGES):
-            stage_tile = keep.tile([P, SIDE], I32, align_bytes=64, name="stage%d" % i)
-            nc.gpsimd.memset(stage_tile[:, BANK:SIDE], 0)
-            stages.append(stage_tile)
-
-        load_x(0)
-        with tc.tile_pool(name="setup", bufs=1) as setup:
-            w_raw = setup.tile([P, PACK, WIDTH], BF16)
-            nc.sync.dma_start(
-                out=w_raw[:].rearrange("p (u e) c -> p u (e c)", u=2),
-                in_=Wq.rearrange("(u p e) c -> p u (e c)", u=2, e=2),
-            )
-            w_grouped = setup.tile([P, WIDTH * PACK], BF16, align_bytes=64)
-            bq_rows = setup.tile([P, P], BF16)
-            nc.vector.memset(bq_rows[:], 0.0)
-            nc.sync.dma_start(out=bq_rows[0:PAIRS, :], in_=bq.rearrange("(h d) -> h d", h=PAIRS))
-            load_x(1)
-            load_keys(0)
-            load_keys(1)
-            load_x(2)
-            turn_x(0, range(JOB_BANKS), ())
-            nc.vector.tensor_copy(
-                out=w_grouped[:].rearrange("p (c t) -> p c t", t=PACK),
-                in_=w_raw[:].rearrange("p t c -> p c t"),
-            )
-            nc.vector.quantize_mx(
-                out=w_codes[:].bitcast(FP8X4), scales=w_scales[:], in_=w_grouped[:]
-            )
-            bq_turned = turn_psum.tile([P, P], BF16, tag="turn")
-            nc.tensor.transpose(bq_turned[:], bq_rows[:], ident_bf16[:])
-            nc.vector.tensor_scalar(
-                out=bias[:], in0=bq_turned[:, 0:PAIRS], scalar1=SCALING, scalar2=None, op0=ALU.mult
-            )
-            turn_x(1, range(JOB_BANKS), ())
-            quantise_x(0)
-            pair_keys(0, 0)
-            pair_keys(0, 1)
-            quantise_x(1)
-
-        q_work = ctx.enter_context(tc.tile_pool(name="q_work", bufs=3))
-        soft = ctx.enter_context(tc.tile_pool(name="soft", bufs=8))
-
-        for rnd in range(ROUNDS):
-            step = rnd // 2
-            if rnd % 2 == 0:
-                if step + 2 < KEY_JOBS:
-                    load_keys(step + 2)
-                if step + 1 < KEY_JOBS:
-                    pair_keys(step + 1, 0)
-            else:
-                if step + 3 < X_JOBS:
-                    load_x(step + 3)
-                if step + 1 < KEY_JOBS:
-                    pair_keys(step + 1, 1)
-            if rnd >= 1:
-                quantise_q(rnd - 1)
-            for pair in range(PAIRS):
-                project_pair(rnd, pair)
-            banks = range(JOB_BANKS)
-            if rnd % 2 == 0:
-                turn_keys(step, banks, KEY_BANKS_ON_VECTOR)
-                if 1 <= step and step + 1 < X_JOBS:
-                    quantise_x(step + 1)
-            else:
-                if step + 2 < X_JOBS:
-                    turn_x(step + 2, banks, X_BANKS_ON_VECTOR)
-                quantise_keys(step)
-            if rnd >= 1:
-                regroup(rnd - 1)
-
-        quantise_q(ROUNDS - 1)
-        regroup(ROUNDS - 1)
+        def attend_store(pair):
+            inverse = soft.tile([P, 2], F32)
+            nc.vector.reciprocal(out=inverse[:], in_=total_of[pair][:])
+            for n in (2 * pair, 2 * pair + 1):
+                it, h = n // HEADS, n % HEADS
+                probs = probs_of[n]
+                nc.gpsimd.tensor_scalar(
+                    out=probs[:], in0=probs[:], scalar1=inverse[:, n % 2 : n % 2 + 1], scalar2=0.0,
+                    op0=ALU.mult, op1=ALU.add,
+                )
+                nc.sync.dma_start(out=out_view[:, h, it, :], in_=probs[:])
 
         maps = COL_TILES * HEADS
-        for n in range(maps + 2):
+        for n in range(maps + 3):
             if n < maps:
                 attend_scores(n)
             if 1 <= n <= maps:
                 attend_exp(n - 1)
-            if n >= 2:
-                attend_store(n - 2)
+            if n >= 3 and n % 2 == 1:
+                attend_store((n - 3) // 2)

@@ -16,299 +16,142 @@ P = 128
 PACK = 4
 BANK = 512
 ROWS, COLS, WIDTH, HEADS, HEAD_DIM = 16, 512, 512, 8, 64
+RUN = 4
 COL_TILES = COLS // P
-HALF_ROWS = 8
-GROUP_ROWS = 4
-HALVES = ROWS // HALF_ROWS
+HALVES = 2
+GROUPS = 2
 PAIRS = HEADS // 2
 SCALING = 1.0 / 32.0
-
-X_JOBS = COL_TILES * HALVES
-KEY_JOBS = HALVES * COL_TILES
-ROUNDS = X_JOBS * 2
-JOB_BANKS = 4
+GROUP_WORK = RUN * WIDTH
 SIDE = BANK + BANK // 4
-VECTOR_BANKS = (0,)
-LOADS_DONE = 10
+STAGES = 4
+STORE_LAG = 6
+MAPS = COL_TILES * HEADS
 
 FLOPS = 2 * ROWS * COLS * WIDTH * WIDTH + 2 * HEADS * COLS * COLS * ROWS * HEAD_DIM
 
 
 def tile_rowselfattention_pa_t_kernel(tc, x, Wq, bq, k, out):
     nc = tc.nc
-    x_view = x[:, :, 0, :].rearrange("r (t p) e -> p t r e", p=P)
-    k_view = k[:, :, 0].rearrange("r (t p) h d -> p t r (h d)", p=P)
+    x_view = x[:, :, 0, :].rearrange(
+        "(half g t) (tile c b) e -> half tile t c g (b e)", half=HALVES, g=GROUPS, tile=COL_TILES, b=RUN
+    )
+    k_view = k[:, :, 0].rearrange(
+        "(half g t) (tile c b) h d -> half tile t c g (b h d)", half=HALVES, g=GROUPS, tile=COL_TILES, b=RUN
+    )
     out_view = out[:, 0].rearrange("h (t p) j -> p h t j", p=P)
 
     with ExitStack() as ctx:
         ctx.enter_context(tc.manual_schedule())
         keep = ctx.enter_context(tc.tile_pool(name="keep", bufs=1))
+        x_in = ctx.enter_context(tc.tile_pool(name="x_in", bufs=3))
+        x_work = ctx.enter_context(tc.tile_pool(name="x_work", bufs=3))
+        soft = ctx.enter_context(tc.tile_pool(name="soft", bufs=8))
         turn_psum = ctx.enter_context(tc.psum_pool(name="turn_psum", bufs=4))
         acc_psum = ctx.enter_context(tc.psum_pool(name="acc_psum", bufs=4))
 
         ident_f32 = keep.tile([P, P], F32)
+        ident_bf16 = keep.tile([P, P], BF16)
         w_codes = keep.tile([P, WIDTH], U32, align_bytes=64)
         w_scales = keep.tile([P, WIDTH], U8, align_bytes=64)
         bias = keep.tile([P, PAIRS], F32)
         k_codes = keep.tile([P, HEADS * HALVES * COLS], U32, align_bytes=64)
         k_scales = keep.tile([P, HEADS * HALVES * COLS], U8, align_bytes=64)
-        q_packed = keep.tile([P, X_JOBS * 3 * SIDE], I32, align_bytes=64)
+        X_JOBS = COL_TILES * HALVES
+        q_packed = keep.tile([P, (2 * X_JOBS + STAGES) * SIDE], I32, align_bytes=64)
 
         def packed_queries(job, part):
-            first = (3 * job + part) * SIDE
-            return q_packed[:, first : first + SIDE]
+            n = 2 * job + part if part < 2 else 2 * X_JOBS + job % STAGES
+            return q_packed[:, n * SIDE : (n + 1) * SIDE]
 
-        with ExitStack() as first_phase:
-            k_in = first_phase.enter_context(tc.tile_pool(name="k_in", bufs=3))
-            x_in = first_phase.enter_context(tc.tile_pool(name="x_in", bufs=3))
-            k_work = first_phase.enter_context(tc.tile_pool(name="k_work", bufs=2))
-            x_work = first_phase.enter_context(tc.tile_pool(name="x_work", bufs=2))
-            x_mx = first_phase.enter_context(tc.tile_pool(name="x_mx", bufs=3))
-            q_work = first_phase.enter_context(tc.tile_pool(name="q_work", bufs=3))
-            x_raw_of, x_grouped_of, x_mx_of = {}, {}, {}
-            k_raw_of, k_pairs_of, k_grouped_of = {}, {}, {}
-            q_grouped_of = {}
-
-            def load_x(job, groups):
-                it, half = job // HALVES, job % HALVES
-                if groups[0] == 0:
-                    x_raw = x_in.tile([P, HALF_ROWS * WIDTH], BF16)
-                    x_raw_of[job] = x_raw
-                first, count = GROUP_ROWS * groups[0], GROUP_ROWS * len(groups)
-                nc.sync.dma_start(
-                    out=x_raw_of[job][:, first * WIDTH : (first + count) * WIDTH].rearrange(
-                        "p (r e) -> p r e", r=count
-                    ),
-                    in_=x_view[:, it, half * HALF_ROWS + first : half * HALF_ROWS + first + count, :],
-                )
-
-            def load_keys(job, groups):
-                half, jt = job // COL_TILES, job % COL_TILES
-                if groups[0] == 0:
-                    k_raw = k_in.tile([P, HALF_ROWS * WIDTH], BF16)
-                    k_raw_of[job] = k_raw
-                first, count = GROUP_ROWS * groups[0], GROUP_ROWS * len(groups)
-                nc.sync.dma_start(
-                    out=k_raw_of[job][:, first * WIDTH : (first + count) * WIDTH].rearrange(
-                        "p (r e) -> p r e", r=count
-                    ),
-                    in_=k_view[:, jt, half * HALF_ROWS + first : half * HALF_ROWS + first + count, :],
-                )
-
-            def empty_bank(on_vector, dst, src):
-                if on_vector:
-                    nc.vector.tensor_copy(out=dst, in_=src)
-                else:
-                    nc.scalar.copy(out=dst, in_=src)
-
-            def turn_x(job, banks, vector_banks):
-                x_words = x_raw_of[job][:].bitcast(F32)
-                if banks[0] == 0:
-                    x_grouped = x_work.tile([P, HALF_ROWS * P * PACK], BF16, align_bytes=64)
-                    x_grouped_of[job] = x_grouped
-                x_grouped_words = x_grouped_of[job][:].bitcast(F32)
-                for bank in banks:
-                    turned = turn_psum.tile([P, 2, 2, P], F32, tag="turn")
-                    for r2 in range(2):
-                        for u in range(2):
-                            first = (2 * bank + r2) * (WIDTH // 2) + u * P
-                            nc.tensor.transpose(
-                                turned[:, r2, u, :], x_words[:, first : first + P], ident_f32[:]
-                            )
-                    empty_bank(
-                        bank in vector_banks,
-                        x_grouped_words[:, bank * BANK : (bank + 1) * BANK].rearrange(
-                            "p (s i u) -> p s i u", s=2, u=2
-                        ),
-                        turned[:].rearrange("p s u i -> p s i u"),
-                    )
-
-            def quantise_x(job, groups):
-                if groups[0] == 0:
-                    x_codes = x_mx.tile([P, HALF_ROWS * P], U32, align_bytes=64)
-                    x_scales = x_mx.tile([P, HALF_ROWS * P], U8, align_bytes=64)
-                    x_mx_of[job] = (x_codes, x_scales)
-                x_codes, x_scales = x_mx_of[job]
-                first, last = BANK * groups[0], BANK * (groups[-1] + 1)
-                nc.vector.quantize_mx(
-                    out=x_codes[:, first:last].bitcast(FP8X4),
-                    scales=x_scales[:, first:last],
-                    in_=x_grouped_of[job][:, first * PACK : last * PACK],
-                )
-
-            def pair_keys(job, a):
-                if a == 0:
-                    k_pairs = k_work.tile([P, HALF_ROWS * WIDTH], BF16)
-                    k_pairs_of[job] = k_pairs
-                nc.vector.tensor_copy(
-                    out=k_pairs_of[job][:].rearrange(
-                        "p (u h a d e) -> p a u h d e", u=2, h=HEADS, a=2, e=2
-                    )[:, a],
-                    in_=k_raw_of[job][:, a * 2048 : (a + 1) * 2048].rearrange(
-                        "p (u e h d) -> p u h d e", u=2, e=2, h=HEADS
-                    ),
-                )
-
-            def turn_keys(job, vector_banks):
-                k_words = k_pairs_of[job][:].bitcast(F32)
-                k_grouped = k_work.tile([P, HEADS * P * PACK], BF16, align_bytes=64)
-                k_grouped_of[job] = k_grouped
-                k_grouped_words = k_grouped[:].bitcast(F32)
-                for bank in range(JOB_BANKS):
-                    turned = turn_psum.tile([P, 2, 2, P], F32, tag="turn")
-                    for h2 in range(2):
-                        for u in range(2):
-                            first = (u * HEADS + 2 * bank + h2) * P
-                            nc.tensor.transpose(
-                                turned[:, h2, u, :], k_words[:, first : first + P], ident_f32[:]
-                            )
-                    empty_bank(
-                        bank in vector_banks,
-                        k_grouped_words[:, bank * BANK : (bank + 1) * BANK].rearrange(
-                            "p (h j u) -> p h j u", h=2, u=2
-                        ),
-                        turned[:].rearrange("p h u j -> p h j u"),
-                    )
-
-            def quantise_keys(job):
-                half, jt = job // COL_TILES, job % COL_TILES
-                for h in range(HEADS):
-                    first = (h * HALVES + half) * COLS + jt * P
-                    nc.vector.quantize_mx(
-                        out=k_codes[:, first : first + P].bitcast(FP8X4),
-                        scales=k_scales[:, first : first + P],
-                        in_=k_grouped_of[job][:, h * P * PACK : (h + 1) * P * PACK],
-                    )
-
-            def project(rnd):
-                job, a = rnd // 2, rnd % 2
-                x_codes, x_scales = x_mx_of[job]
-                q_grouped = q_work.tile([P, PAIRS * P * PACK], BF16, align_bytes=64)
-                q_grouped_of[rnd] = q_grouped
-                for pair in range(PAIRS):
-                    q_acc = acc_psum.tile([P, BANK], F32, tag="acc")
-                    nc.tensor.matmul_mx(
-                        out=q_acc[:],
-                        lhsT=w_codes[:, pair * P : (pair + 1) * P].bitcast(FP8X4),
-                        lhsT_scale=w_scales[:, pair * P : (pair + 1) * P],
-                        rhs=x_codes[:, a * BANK : (a + 1) * BANK].bitcast(FP8X4),
-                        rhs_scale=x_scales[:, a * BANK : (a + 1) * BANK],
-                        start=True,
-                        stop=True,
-                    )
-                    nc.scalar.activation(
-                        out=q_grouped[:, pair * BANK : (pair + 1) * BANK].rearrange(
-                            "p (i t) -> p i t", t=PACK
-                        ),
-                        in_=q_acc[:].rearrange("p (t i) -> p i t", t=PACK),
-                        func=ACT.Identity,
-                        bias=bias[:, pair : pair + 1],
-                        scale=SCALING,
-                    )
-
-            def quantise_q(rnd):
-                job, a = rnd // 2, rnd % 2
-                packed = packed_queries(job, 2 * a)
-                nc.vector.quantize_mx(
-                    out=packed[:, 0:BANK].bitcast(FP8X4),
-                    scales=packed[:, BANK:SIDE].bitcast(U8),
-                    in_=q_grouped_of[rnd][:],
-                )
-
-            def regroup(job):
-                even, odd, both = (packed_queries(job, part) for part in range(3))
-                nc.sync.dma_start(out=odd[0:HEAD_DIM, :], in_=even[HEAD_DIM:P, :])
-                nc.sync.dma_start(out=odd[HEAD_DIM:P, :], in_=both[HEAD_DIM:P, :])
-                nc.sync.dma_start(out=even[HEAD_DIM:P, :], in_=both[0:HEAD_DIM, :])
-
-            with tc.tile_pool(name="setup", bufs=1) as setup:
-                w_raw = setup.tile([P, PACK, WIDTH], BF16)
-                nc.sync.dma_start(
-                    out=w_raw[:].rearrange("p (u e) c -> p u (e c)", u=2),
-                    in_=Wq.rearrange("(u p e) c -> p u (e c)", u=2, e=2),
-                )
-                load_x(0, (0,))
-                load_x(0, (1,))
-                bq_rows = setup.tile([P, P], BF16)
-                nc.vector.memset(bq_rows[:], 0.0)
-                nc.sync.dma_start(
-                    out=bq_rows[0:PAIRS, :], in_=bq.rearrange("(h d) -> h d", h=PAIRS)
-                )
-                load_keys(0, (0,))
-                load_keys(0, (1,))
-                load_x(1, (0, 1))
-                load_keys(1, (0, 1))
-                make_identity(nc, ident_f32[:])
-                ident_bf16 = setup.tile([P, P], BF16)
-                make_identity(nc, ident_bf16[:])
-                nc.gpsimd.memset(
-                    q_packed[:].rearrange("p (n w) -> p n w", w=SIDE)[:, :, BANK:SIDE], 0
-                )
-                w_grouped = setup.tile([P, WIDTH * PACK], BF16, align_bytes=64)
-                nc.vector.tensor_copy(
-                    out=w_grouped[:].rearrange("p (c t) -> p c t", t=PACK),
-                    in_=w_raw[:].rearrange("p t c -> p c t"),
-                )
-                nc.vector.quantize_mx(
-                    out=w_codes[:].bitcast(FP8X4), scales=w_scales[:], in_=w_grouped[:]
-                )
-                turn_x(0, (0, 1), (0,))
-                quantise_x(0, (0,))
-                bq_turned = acc_psum.tile([P, P], BF16, tag="acc")
-                nc.tensor.transpose(bq_turned[:], bq_rows[:], ident_bf16[:])
-                nc.vector.tensor_scalar(
-                    out=bias[:],
-                    in0=bq_turned[:, 0:PAIRS],
-                    scalar1=SCALING,
-                    scalar2=None,
-                    op0=ALU.mult,
-                )
-                turn_x(0, (2, 3), (2,))
-                quantise_x(0, (1,))
-                pair_keys(0, 0)
-
-            x_turn = {2 * job - 2: job for job in range(1, X_JOBS)}
-            k_turn = {2 * job + 1: job for job in range(KEY_JOBS - 1)}
-            k_turn[ROUNDS - 2] = KEY_JOBS - 1
-            moved = 0
-            for rnd in range(ROUNDS + 1):
-                if rnd % 2 == 0:
-                    if rnd == 0:
-                        project(rnd)
-                    if rnd // 2 < KEY_JOBS:
-                        pair_keys(rnd // 2, 1)
-                    if rnd in x_turn:
-                        turn_x(x_turn[rnd], range(JOB_BANKS), VECTOR_BANKS)
-                    if rnd in k_turn:
-                        turn_keys(k_turn[rnd], VECTOR_BANKS)
-                    if 0 < rnd < ROUNDS:
-                        project(rnd)
-                    if rnd >= 1:
-                        quantise_q(rnd - 1)
-                    if rnd - 1 in k_turn:
-                        quantise_keys(k_turn[rnd - 1])
-                else:
-                    project(rnd)
-                    if rnd - 1 in x_turn:
-                        quantise_x(x_turn[rnd - 1], (0, 1))
-                    if rnd // 2 + 1 < KEY_JOBS:
-                        pair_keys(rnd // 2 + 1, 0)
-                    quantise_q(rnd - 1)
-                    if rnd in k_turn:
-                        turn_keys(k_turn[rnd], VECTOR_BANKS)
-                    if rnd - 1 in k_turn:
-                        quantise_keys(k_turn[rnd - 1])
-                if rnd % 2 == 0 and rnd // 2 + 2 < X_JOBS:
-                    load_x(rnd // 2 + 2, (0, 1))
-                    load_keys(rnd // 2 + 2, (0, 1))
-                if rnd >= LOADS_DONE:
-                    while 2 * moved + 1 < rnd:
-                        regroup(moved)
-                        moved += 1
-
-        soft = ctx.enter_context(tc.tile_pool(name="soft", bufs=8))
-        probs_pool = ctx.enter_context(tc.tile_pool(name="probs_pool", bufs=16))
+        x_raw_of, x_grouped_of, x_mx_of, q_grouped_of = {}, {}, {}, {}
+        k_raw_of, k_by_head_of, k_grouped_of = {}, {}, {}
         scores_of, probs_of, total_of = {}, {}, {}
+
+        def load(tile, view, half, col_tile, first=0, last=GROUPS):
+            for t in range(PACK):
+                nc.sync.dma_start(
+                    out=tile[t:P:PACK, first * GROUP_WORK : last * GROUP_WORK].rearrange(
+                        "p (g f) -> p g f", f=GROUP_WORK
+                    ),
+                    in_=view[half, col_tile, t][:, first:last],
+                )
+
+        def load_x(job):
+            x_raw = x_in.tile([P, GROUPS * GROUP_WORK], BF16)
+            x_raw_of[job] = x_raw
+            if job > 0:
+                load(x_raw, x_view, job % HALVES, job // HALVES)
+
+        def turn_x(job, g):
+            x_words = x_raw_of[job][:].bitcast(F32)
+            x_grouped = x_work.tile([P, GROUP_WORK], BF16, align_bytes=64)
+            x_grouped_of[job, g] = x_grouped
+            x_grouped_words = x_grouped[:].bitcast(F32)
+            for bank in range(2):
+                turned = turn_psum.tile([P, 2, 2, P], F32, tag="turn")
+                for s in range(2):
+                    for u in range(2):
+                        first = (g * RUN + 2 * bank + s) * (WIDTH // 2) + u * P
+                        nc.tensor.transpose(
+                            turned[:, s, u, :], x_words[:, first : first + P], ident_f32[:]
+                        )
+                (nc.scalar.copy if 2 * job + g < 5 else nc.vector.tensor_copy)(
+                    out=x_grouped_words[:, bank * BANK : (bank + 1) * BANK].rearrange(
+                        "p (s c u) -> p s c u", s=2, u=2
+                    ),
+                    in_=turned[:].rearrange("p s u c -> p s c u"),
+                )
+
+        def quantise_x(job, g):
+            x_codes = x_work.tile([P, BANK], U32, align_bytes=64)
+            x_scales = x_work.tile([P, BANK], U8, align_bytes=64)
+            x_mx_of[job, g] = (x_codes, x_scales)
+            nc.vector.quantize_mx(
+                out=x_codes[:].bitcast(FP8X4), scales=x_scales[:], in_=x_grouped_of[job, g][:]
+            )
+
+        def project(job, g):
+            x_codes, x_scales = x_mx_of[job, g]
+            q_grouped = x_work.tile([P, PAIRS * BANK], BF16, align_bytes=64)
+            q_grouped_of[job, g] = q_grouped
+            for pair in range(PAIRS):
+                q_acc = acc_psum.tile([P, BANK], F32, tag="acc")
+                nc.tensor.matmul_mx(
+                    out=q_acc[:],
+                    lhsT=w_codes[:, pair * P : (pair + 1) * P].bitcast(FP8X4),
+                    lhsT_scale=w_scales[:, pair * P : (pair + 1) * P],
+                    rhs=x_codes[:].bitcast(FP8X4),
+                    rhs_scale=x_scales[:],
+                    start=True,
+                    stop=True,
+                )
+                nc.scalar.activation(
+                    out=q_grouped[:, pair * BANK : (pair + 1) * BANK].rearrange(
+                        "p (c b t) -> p c b t", b=RUN, t=PACK
+                    ),
+                    in_=q_acc[:].rearrange("p (b c t) -> p c b t", b=RUN, t=PACK),
+                    func=ACT.Identity,
+                    bias=bias[:, pair : pair + 1],
+                    scale=SCALING,
+                )
+
+        def quantise_q(job, g):
+            packed = packed_queries(job, 2 * g)
+            nc.vector.quantize_mx(
+                out=packed[:, 0:BANK].bitcast(FP8X4),
+                scales=packed[:, BANK:SIDE].bitcast(U8),
+                in_=q_grouped_of[job, g][:],
+            )
+
+        def regroup(job, step):
+            even, odd, both = (packed_queries(job, part) for part in range(3))
+            if step == 0:
+                nc.sync.dma_start(out=odd[0:HEAD_DIM, :], in_=even[HEAD_DIM:P, :])
+            elif step == 1:
+                nc.sync.dma_start(out=odd[HEAD_DIM:P, :], in_=both[HEAD_DIM:P, :])
+            else:
+                nc.sync.dma_start(out=even[HEAD_DIM:P, :], in_=both[0:HEAD_DIM, :])
 
         def attend_scores(n):
             it, h = n // HEADS, n % HEADS
@@ -326,11 +169,15 @@ def tile_rowselfattention_pa_t_kernel(tc, x, Wq, bq, k, out):
                     start=(half == 0),
                     stop=(half == HALVES - 1),
                 )
+            scores_of[n] = scores
+
+        def attend_max(n):
             neg_max = soft.tile([P, 1], F32)
             nc.vector.tensor_reduce(
-                out=neg_max[:], in_=scores[:], axis=mybir.AxisListType.X, op=ALU.max, negate=True
+                out=neg_max[:], in_=scores_of[n][:], axis=mybir.AxisListType.X, op=ALU.max,
+                negate=True,
             )
-            scores_of[n] = (scores, neg_max)
+            scores_of[n] = (scores_of[n], neg_max)
 
         def attend_exp(n):
             scores, neg_max = scores_of[n]
@@ -339,28 +186,204 @@ def tile_rowselfattention_pa_t_kernel(tc, x, Wq, bq, k, out):
                 total = soft.tile([P, 2], F32)
                 total_of[n // 2] = total
             nc.scalar.activation(
-                out=probs[:], in_=scores[:], func=ACT.Exp, bias=neg_max[:, 0:1], scale=1.0,
+                out=probs[:].rearrange("p (tile c b) -> p tile c b", b=RUN, tile=COL_TILES),
+                in_=scores[:].rearrange("p (tile b c) -> p tile c b", b=RUN, tile=COL_TILES),
+                func=ACT.Exp,
+                bias=neg_max[:, 0:1],
+                scale=1.0,
                 accum_out=total_of[n // 2][:, n % 2 : n % 2 + 1],
             )
             probs_of[n] = probs
 
-        def attend_store(pair):
+        def attend_inverse(pair):
             inverse = soft.tile([P, 2], F32)
             nc.vector.reciprocal(out=inverse[:], in_=total_of[pair][:])
+            total_of[pair] = inverse
+
+        def attend_normalise(pair):
+            inverse = total_of[pair]
             for n in (2 * pair, 2 * pair + 1):
                 it, h = n // HEADS, n % HEADS
                 probs = probs_of[n]
-                nc.gpsimd.tensor_scalar(
+                on_vector = n >= 16 and n % 4 == 3
+                engine = nc.vector if on_vector else nc.gpsimd
+                engine.tensor_scalar(
                     out=probs[:], in0=probs[:], scalar1=inverse[:, n % 2 : n % 2 + 1], scalar2=0.0,
                     op0=ALU.mult, op1=ALU.add,
                 )
-                nc.sync.dma_start(out=out_view[:, h, it, :], in_=probs[:])
 
-        maps = COL_TILES * HEADS
-        for n in range(maps + 3):
-            if n < maps:
-                attend_scores(n)
-            if 1 <= n <= maps:
-                attend_exp(n - 1)
-            if n >= 3 and n % 2 == 1:
-                attend_store((n - 3) // 2)
+        def store(n):
+            it, h = n // HEADS, n % HEADS
+            nc.sync.dma_start(out=out_view[:, h, it, :], in_=probs_of[n][:])
+
+        def x_piece(n):
+            return ("x", n // GROUPS, n % GROUPS)
+
+        def key_job(n):
+            return ("k", n, 0)
+
+        items = [x_piece(0)]
+        for n in range(8):
+            items.append(x_piece(n + 1))
+            items.append(key_job(n))
+        KEYS_DONE = len(items) + 1
+        for n in range(9, 16):
+            items.append(x_piece(n))
+        state = {"map": 0}
+
+        def reload_x(tick):
+            freed = item_at(tick - 1, "x")
+            if freed and freed[1] == 1 and freed[0] + 3 < X_JOBS:
+                load_x(freed[0] + 3)
+
+        def item_at(tick, kind):
+            if 0 <= tick < len(items) and items[tick][0] == kind:
+                return items[tick][1:]
+            return None
+
+        def attend(count):
+            for c in range(count):
+                n = state["map"]
+                if n < MAPS:
+                    attend_scores(n)
+                    attend_max(n)
+                if 1 <= n <= MAPS:
+                    attend_exp(n - 1)
+                if 3 <= n <= MAPS + 2 and n % 2 == 1:
+                    attend_inverse((n - 3) // 2)
+                if 4 <= n <= MAPS + 3 and n % 2 == 0:
+                    attend_normalise((n - 4) // 2)
+                if 0 <= n - STORE_LAG < MAPS:
+                    store(n - STORE_LAG)
+                state["map"] = n + 1
+
+        def finish_queries(tick):
+            done = item_at(tick - 3, "x")
+            if done:
+                quantise_q(*done)
+            done = item_at(tick - 4, "x")
+            if done:
+                regroup(done[0], done[1])
+            done = item_at(tick - 5, "x")
+            if done and done[1] == 1:
+                regroup(done[0], 2)
+
+        with ExitStack() as key_phase:
+            k_in = key_phase.enter_context(tc.tile_pool(name="k_in", bufs=3))
+            k_work = key_phase.enter_context(tc.tile_pool(name="k_work", bufs=2))
+
+            def load_keys(job):
+                k_raw = k_in.tile([P, GROUPS * GROUP_WORK], BF16)
+                load(k_raw, k_view, job // COL_TILES, job % COL_TILES)
+                k_raw_of[job] = k_raw
+
+            def order_keys(job):
+                k_by_head = k_work.tile([P, GROUPS * GROUP_WORK], BF16)
+                k_by_head_of[job] = k_by_head
+                nc.vector.tensor_copy(
+                    out=k_by_head[:].rearrange("p (n g d) -> p n g d", g=GROUPS, d=HEAD_DIM),
+                    in_=k_raw_of[job][:].rearrange("p (g n d) -> p n g d", g=GROUPS, d=HEAD_DIM),
+                )
+
+            def turn_keys(job):
+                k_grouped = k_work.tile([P, GROUPS * GROUP_WORK], BF16, align_bytes=64)
+                k_grouped_of[job] = k_grouped
+                k_by_head = k_by_head_of[job]
+                for bank in range(4):
+                    turned = turn_psum.tile([P, 8, P], BF16, tag="turn")
+                    for s in range(8):
+                        h, b = 2 * bank + s // RUN, s % RUN
+                        first = (b * HEADS + h) * P
+                        nc.tensor.transpose(
+                            turned[:, s, :], k_by_head[:, first : first + P], ident_bf16[:]
+                        )
+                    nc.scalar.copy(
+                        out=k_grouped[:, bank * 1024 : (bank + 1) * 1024].bitcast(F32),
+                        in_=turned[:].rearrange("p s c -> p (s c)").bitcast(F32),
+                    )
+
+            def quantise_keys(job):
+                half, tile = job // COL_TILES, job % COL_TILES
+                for h in range(HEADS):
+                    first = (h * HALVES + half) * COLS + tile * P
+                    nc.vector.quantize_mx(
+                        out=k_codes[:, first : first + P].bitcast(FP8X4),
+                        scales=k_scales[:, first : first + P],
+                        in_=k_grouped_of[job][:, h * BANK : (h + 1) * BANK],
+                    )
+
+            with tc.tile_pool(name="setup", bufs=1) as setup:
+                load_x(0)
+                load(x_raw_of[0], x_view, 0, 0, 0, 1)
+                w_raw = setup.tile([P, PACK, WIDTH], BF16)
+                nc.sync.dma_start(
+                    out=w_raw[:].rearrange("p (u e) c -> p u (e c)", u=2),
+                    in_=Wq.rearrange("(u p e) c -> p u (e c)", u=2, e=2),
+                )
+                bq_rows = setup.tile([P, P], BF16)
+                nc.vector.memset(bq_rows[:], 0.0)
+                load(x_raw_of[0], x_view, 0, 0, 1, 2)
+                nc.sync.dma_start(
+                    out=bq_rows[0:PAIRS, :], in_=bq.rearrange("(h d) -> h d", h=PAIRS)
+                )
+                load_keys(0)
+                load_keys(1)
+                load_x(1)
+                load_keys(2)
+                load_x(2)
+                make_identity(nc, ident_f32[:])
+                make_identity(nc, ident_bf16[:])
+                nc.gpsimd.memset(
+                    q_packed[:].rearrange("p (n w) -> p n w", w=SIDE)[:, :, BANK:SIDE], 0
+                )
+                w_grouped = setup.tile([P, WIDTH * PACK], BF16, align_bytes=64)
+                nc.vector.tensor_copy(
+                    out=w_grouped[:].rearrange("p (c t) -> p c t", t=PACK),
+                    in_=w_raw[:].rearrange("p t c -> p c t"),
+                )
+                nc.vector.quantize_mx(
+                    out=w_codes[:].bitcast(FP8X4), scales=w_scales[:], in_=w_grouped[:]
+                )
+                turn_x(0, 0)
+                bq_turned = acc_psum.tile([P, P], BF16, tag="acc")
+                nc.tensor.transpose(bq_turned[:], bq_rows[:], ident_bf16[:])
+                nc.vector.tensor_scalar(
+                    out=bias[:],
+                    in0=bq_turned[:, 0:PAIRS],
+                    scalar1=SCALING,
+                    scalar2=None,
+                    op0=ALU.mult,
+                )
+
+            for tick in range(KEYS_DONE):
+                if tick >= 1 and item_at(tick, "k") and item_at(tick, "k")[0] + 3 < 8:
+                    load_keys(item_at(tick, "k")[0] + 3)
+                reload_x(tick)
+                if tick >= 3 and item_at(tick + 1, "k"):
+                    order_keys(item_at(tick + 1, "k")[0])
+                if item_at(tick, "k"):
+                    turn_keys(item_at(tick, "k")[0])
+                if tick > 0 and item_at(tick, "x"):
+                    turn_x(*item_at(tick, "x"))
+                if item_at(tick - 2, "x"):
+                    project(*item_at(tick - 2, "x"))
+                if item_at(tick - 1, "k"):
+                    quantise_keys(item_at(tick - 1, "k")[0])
+                if item_at(tick - 1, "x"):
+                    quantise_x(*item_at(tick - 1, "x"))
+                finish_queries(tick)
+                if tick < 3 and item_at(tick + 1, "k"):
+                    order_keys(item_at(tick + 1, "k")[0])
+
+        probs_pool = ctx.enter_context(tc.tile_pool(name="probs_pool", bufs=12))
+        for tick in range(KEYS_DONE, len(items) + 7):
+            reload_x(tick)
+            if item_at(tick, "x"):
+                turn_x(*item_at(tick, "x"))
+            if item_at(tick - 2, "x"):
+                project(*item_at(tick - 2, "x"))
+            finish_queries(tick)
+            if item_at(tick - 1, "x"):
+                quantise_x(*item_at(tick - 1, "x"))
+            attend(2)
+        attend(MAPS + STORE_LAG - state["map"])

@@ -24,9 +24,12 @@ PAIRS = HEADS // 2
 SCALING = 1.0 / 32.0
 GROUP_WORK = RUN * WIDTH
 SIDE = BANK + BANK // 4
-STAGES = 4
+KEY_SIDE = 2 * P
 STORE_LAG = 6
+LOADS_DONE = 16
 MAPS = COL_TILES * HEADS
+X_JOBS = COL_TILES * HALVES
+KEY_JOBS = COL_TILES * HALVES
 
 FLOPS = 2 * ROWS * COLS * WIDTH * WIDTH + 2 * HEADS * COLS * COLS * ROWS * HEAD_DIM
 
@@ -57,11 +60,10 @@ def tile_rowselfattention_pa_t_kernel(tc, x, Wq, bq, k, out):
         bias = keep.tile([P, PAIRS], F32)
         k_codes = keep.tile([P, HEADS * HALVES * COLS], U32, align_bytes=64)
         k_scales = keep.tile([P, HEADS * HALVES * COLS], U8, align_bytes=64)
-        X_JOBS = COL_TILES * HALVES
-        q_packed = keep.tile([P, (2 * X_JOBS + STAGES) * SIDE], I32, align_bytes=64)
+        q_packed = keep.tile([P, 3 * X_JOBS * SIDE], I32, align_bytes=64)
 
         def packed_queries(job, part):
-            n = 2 * job + part if part < 2 else 2 * X_JOBS + job % STAGES
+            n = 3 * job + part
             return q_packed[:, n * SIDE : (n + 1) * SIDE]
 
         x_raw_of, x_grouped_of, x_mx_of, q_grouped_of = {}, {}, {}, {}
@@ -96,7 +98,7 @@ def tile_rowselfattention_pa_t_kernel(tc, x, Wq, bq, k, out):
                         nc.tensor.transpose(
                             turned[:, s, u, :], x_words[:, first : first + P], ident_f32[:]
                         )
-                (nc.scalar.copy if 2 * job + g < 5 else nc.vector.tensor_copy)(
+                (nc.scalar.copy if 2 * job + g < 2 else nc.vector.tensor_copy)(
                     out=x_grouped_words[:, bank * BANK : (bank + 1) * BANK].rearrange(
                         "p (s c u) -> p s c u", s=2, u=2
                     ),
@@ -156,16 +158,16 @@ def tile_rowselfattention_pa_t_kernel(tc, x, Wq, bq, k, out):
         def attend_scores(n):
             it, h = n // HEADS, n % HEADS
             scores = acc_psum.tile([P, COLS], F32, tag="acc")
-            for half in range(HALVES):
+            for side, half in ((0, 0), (0, 1), (1, 0), (1, 1)):
                 packed = packed_queries(it * HALVES + half, h % 2)
                 q_first = (h // 2) * P
-                k_first = (h * HALVES + half) * COLS
+                k_first = ((half * 2 + side) * HEADS + h) * KEY_SIDE
                 nc.tensor.matmul_mx(
-                    out=scores[:],
+                    out=scores[:, side * KEY_SIDE : (side + 1) * KEY_SIDE],
                     lhsT=packed[:, q_first : q_first + P].bitcast(FP8X4),
                     lhsT_scale=packed[:, BANK:SIDE].bitcast(U8)[:, q_first : q_first + P],
-                    rhs=k_codes[:, k_first : k_first + COLS].bitcast(FP8X4),
-                    rhs_scale=k_scales[:, k_first : k_first + COLS],
+                    rhs=k_codes[:, k_first : k_first + KEY_SIDE].bitcast(FP8X4),
+                    rhs_scale=k_scales[:, k_first : k_first + KEY_SIDE],
                     start=(half == 0),
                     stop=(half == HALVES - 1),
                 )
@@ -205,8 +207,12 @@ def tile_rowselfattention_pa_t_kernel(tc, x, Wq, bq, k, out):
             for n in (2 * pair, 2 * pair + 1):
                 it, h = n // HEADS, n % HEADS
                 probs = probs_of[n]
-                on_vector = n >= 16 and n % 4 == 3
-                engine = nc.vector if on_vector else nc.gpsimd
+                if n % 8 == 7:
+                    nc.scalar.activation(
+                        out=probs[:], in_=probs[:], func=ACT.Copy, scale=inverse[:, n % 2 : n % 2 + 1]
+                    )
+                    continue
+                engine = nc.vector if n % 8 == 3 else nc.gpsimd
                 engine.tensor_scalar(
                     out=probs[:], in0=probs[:], scalar1=inverse[:, n % 2 : n % 2 + 1], scalar2=0.0,
                     op0=ALU.mult, op1=ALU.add,
@@ -222,13 +228,11 @@ def tile_rowselfattention_pa_t_kernel(tc, x, Wq, bq, k, out):
         def key_job(n):
             return ("k", n, 0)
 
-        items = [x_piece(0)]
-        for n in range(8):
-            items.append(x_piece(n + 1))
+        items = [x_piece(0), x_piece(1)]
+        for n in range(KEY_JOBS):
             items.append(key_job(n))
-        KEYS_DONE = len(items) + 1
-        for n in range(9, 16):
-            items.append(x_piece(n))
+            for m in range(2 * n + 2, min(2 * n + 4, 2 * X_JOBS)):
+                items.append(x_piece(m))
         state = {"map": 0}
 
         def reload_x(tick):
@@ -257,20 +261,10 @@ def tile_rowselfattention_pa_t_kernel(tc, x, Wq, bq, k, out):
                     store(n - STORE_LAG)
                 state["map"] = n + 1
 
-        def finish_queries(tick):
-            done = item_at(tick - 3, "x")
-            if done:
-                quantise_q(*done)
-            done = item_at(tick - 4, "x")
-            if done:
-                regroup(done[0], done[1])
-            done = item_at(tick - 5, "x")
-            if done and done[1] == 1:
-                regroup(done[0], 2)
-
         with ExitStack() as key_phase:
             k_in = key_phase.enter_context(tc.tile_pool(name="k_in", bufs=3))
-            k_work = key_phase.enter_context(tc.tile_pool(name="k_work", bufs=2))
+            k_order = key_phase.enter_context(tc.tile_pool(name="k_order", bufs=2))
+            k_work = key_phase.enter_context(tc.tile_pool(name="k_work", bufs=1))
 
             def load_keys(job):
                 k_raw = k_in.tile([P, GROUPS * GROUP_WORK], BF16)
@@ -278,7 +272,7 @@ def tile_rowselfattention_pa_t_kernel(tc, x, Wq, bq, k, out):
                 k_raw_of[job] = k_raw
 
             def order_keys(job):
-                k_by_head = k_work.tile([P, GROUPS * GROUP_WORK], BF16)
+                k_by_head = k_order.tile([P, GROUPS * GROUP_WORK], BF16)
                 k_by_head_of[job] = k_by_head
                 nc.vector.tensor_copy(
                     out=k_by_head[:].rearrange("p (n g d) -> p n g d", g=GROUPS, d=HEAD_DIM),
@@ -286,8 +280,13 @@ def tile_rowselfattention_pa_t_kernel(tc, x, Wq, bq, k, out):
                 )
 
             def turn_keys(job):
-                k_grouped = k_work.tile([P, GROUPS * GROUP_WORK], BF16, align_bytes=64)
-                k_grouped_of[job] = k_grouped
+                if job % 2 == 0:
+                    k_grouped = k_work.tile([P, 2 * GROUPS * GROUP_WORK], BF16, align_bytes=64)
+                    k_grouped_of[job // 2] = k_grouped
+                k_grouped = k_grouped_of[job // 2]
+                k_grouped_words = k_grouped[:].bitcast(F32).rearrange(
+                    "p (h n) -> p h n", h=HEADS
+                )[:, :, job % 2 * 256 : (job % 2 + 1) * 256]
                 k_by_head = k_by_head_of[job]
                 for bank in range(4):
                     turned = turn_psum.tile([P, 8, P], BF16, tag="turn")
@@ -298,19 +297,20 @@ def tile_rowselfattention_pa_t_kernel(tc, x, Wq, bq, k, out):
                             turned[:, s, :], k_by_head[:, first : first + P], ident_bf16[:]
                         )
                     nc.scalar.copy(
-                        out=k_grouped[:, bank * 1024 : (bank + 1) * 1024].bitcast(F32),
-                        in_=turned[:].rearrange("p s c -> p (s c)").bitcast(F32),
+                        out=k_grouped_words[:, 2 * bank : 2 * bank + 2, :],
+                        in_=turned[:]
+                        .rearrange("p s c -> p (s c)")
+                        .bitcast(F32)
+                        .rearrange("p (h n) -> p h n", h=2),
                     )
 
-            def quantise_keys(job):
-                half, tile = job // COL_TILES, job % COL_TILES
-                for h in range(HEADS):
-                    first = (h * HALVES + half) * COLS + tile * P
-                    nc.vector.quantize_mx(
-                        out=k_codes[:, first : first + P].bitcast(FP8X4),
-                        scales=k_scales[:, first : first + P],
-                        in_=k_grouped_of[job][:, h * BANK : (h + 1) * BANK],
-                    )
+            def quantise_keys(job, part):
+                first = ((job // 2) * HEADS + 4 * part) * KEY_SIDE
+                nc.vector.quantize_mx(
+                    out=k_codes[:, first : first + 4 * KEY_SIDE].bitcast(FP8X4),
+                    scales=k_scales[:, first : first + 4 * KEY_SIDE],
+                    in_=k_grouped_of[job // 2][:, part * 4096 : (part + 1) * 4096],
+                )
 
             with tc.tile_pool(name="setup", bufs=1) as setup:
                 load_x(0)
@@ -327,10 +327,10 @@ def tile_rowselfattention_pa_t_kernel(tc, x, Wq, bq, k, out):
                     out=bq_rows[0:PAIRS, :], in_=bq.rearrange("(h d) -> h d", h=PAIRS)
                 )
                 load_keys(0)
-                load_keys(1)
                 load_x(1)
-                load_keys(2)
+                load_keys(1)
                 load_x(2)
+                load_keys(2)
                 make_identity(nc, ident_f32[:])
                 make_identity(nc, ident_bf16[:])
                 nc.gpsimd.memset(
@@ -355,35 +355,49 @@ def tile_rowselfattention_pa_t_kernel(tc, x, Wq, bq, k, out):
                     op0=ALU.mult,
                 )
 
-            for tick in range(KEYS_DONE):
-                if tick >= 1 and item_at(tick, "k") and item_at(tick, "k")[0] + 3 < 8:
-                    load_keys(item_at(tick, "k")[0] + 3)
-                reload_x(tick)
-                if tick >= 3 and item_at(tick + 1, "k"):
-                    order_keys(item_at(tick + 1, "k")[0])
+            ready, half_moved = [], []
+            for tick in range(len(items) + 5):
+                keys, piece = item_at(tick - 1, "k"), item_at(tick - 1, "x")
+                if keys and keys[0] + 3 < KEY_JOBS:
+                    load_keys(keys[0] + 3)
+                if piece and piece[1] == 1 and piece[0] + 3 < X_JOBS:
+                    load_x(piece[0] + 3)
+                if tick >= 2 and item_at(tick + 2, "k"):
+                    order_keys(item_at(tick + 2, "k")[0])
+                if tick == 2:
+                    project(0, 0)
                 if item_at(tick, "k"):
                     turn_keys(item_at(tick, "k")[0])
                 if tick > 0 and item_at(tick, "x"):
                     turn_x(*item_at(tick, "x"))
-                if item_at(tick - 2, "x"):
+                if tick > 2 and item_at(tick - 2, "x"):
                     project(*item_at(tick - 2, "x"))
-                if item_at(tick - 1, "k"):
-                    quantise_keys(item_at(tick - 1, "k")[0])
                 if item_at(tick - 1, "x"):
                     quantise_x(*item_at(tick - 1, "x"))
-                finish_queries(tick)
-                if tick < 3 and item_at(tick + 1, "k"):
-                    order_keys(item_at(tick + 1, "k")[0])
+                for part in range(2):
+                    keys = item_at(tick - 1 - part, "k")
+                    if keys and keys[0] % 2 == 1:
+                        quantise_keys(keys[0], part)
+                if tick >= LOADS_DONE:
+                    for job in half_moved:
+                        regroup(job, 2)
+                    for job in ready:
+                        regroup(job, 0)
+                        regroup(job, 1)
+                    half_moved, ready = ready, []
+                piece = item_at(tick - 4, "x")
+                if piece:
+                    quantise_q(*piece)
+                    if piece[1] == 1:
+                        ready.append(piece[0])
+                if tick == 1:
+                    order_keys(0)
+            for job in half_moved:
+                regroup(job, 2)
+            for job in ready:
+                regroup(job, 0)
+                regroup(job, 1)
+                regroup(job, 2)
 
-        probs_pool = ctx.enter_context(tc.tile_pool(name="probs_pool", bufs=12))
-        for tick in range(KEYS_DONE, len(items) + 7):
-            reload_x(tick)
-            if item_at(tick, "x"):
-                turn_x(*item_at(tick, "x"))
-            if item_at(tick - 2, "x"):
-                project(*item_at(tick - 2, "x"))
-            finish_queries(tick)
-            if item_at(tick - 1, "x"):
-                quantise_x(*item_at(tick - 1, "x"))
-            attend(2)
-        attend(MAPS + STORE_LAG - state["map"])
+        probs_pool = ctx.enter_context(tc.tile_pool(name="probs_pool", bufs=16))
+        attend(MAPS + STORE_LAG)

@@ -25,11 +25,12 @@ SCALING = 1.0 / 32.0
 GROUP_WORK = RUN * WIDTH
 SIDE = BANK + BANK // 4
 KEY_SIDE = 2 * P
-STORE_LAG = 6
-LOADS_DONE = 16
 MAPS = COL_TILES * HEADS
 X_JOBS = COL_TILES * HALVES
 KEY_JOBS = COL_TILES * HALVES
+STORE_LAG = 6
+STAGES = 4
+XV = ((0, 1), (0, 1))
 
 FLOPS = 2 * ROWS * COLS * WIDTH * WIDTH + 2 * HEADS * COLS * COLS * ROWS * HEAD_DIM
 
@@ -47,9 +48,6 @@ def tile_rowselfattention_pa_t_kernel(tc, x, Wq, bq, k, out):
     with ExitStack() as ctx:
         ctx.enter_context(tc.manual_schedule())
         keep = ctx.enter_context(tc.tile_pool(name="keep", bufs=1))
-        x_in = ctx.enter_context(tc.tile_pool(name="x_in", bufs=3))
-        x_work = ctx.enter_context(tc.tile_pool(name="x_work", bufs=3))
-        soft = ctx.enter_context(tc.tile_pool(name="soft", bufs=8))
         turn_psum = ctx.enter_context(tc.psum_pool(name="turn_psum", bufs=4))
         acc_psum = ctx.enter_context(tc.psum_pool(name="acc_psum", bufs=4))
 
@@ -60,216 +58,122 @@ def tile_rowselfattention_pa_t_kernel(tc, x, Wq, bq, k, out):
         bias = keep.tile([P, PAIRS], F32)
         k_codes = keep.tile([P, HEADS * HALVES * COLS], U32, align_bytes=64)
         k_scales = keep.tile([P, HEADS * HALVES * COLS], U8, align_bytes=64)
-        q_packed = keep.tile([P, 3 * X_JOBS * SIDE], I32, align_bytes=64)
+        q_packed = keep.tile([P, (2 * X_JOBS + STAGES) * SIDE], I32, align_bytes=64)
 
         def packed_queries(job, part):
-            n = 3 * job + part
+            n = 2 * job + part if part < 2 else 2 * X_JOBS + job % STAGES
             return q_packed[:, n * SIDE : (n + 1) * SIDE]
 
-        x_raw_of, x_grouped_of, x_mx_of, q_grouped_of = {}, {}, {}, {}
-        k_raw_of, k_by_head_of, k_grouped_of = {}, {}, {}
-        scores_of, probs_of, total_of = {}, {}, {}
+        with ExitStack() as first_phase:
+            x_in = first_phase.enter_context(tc.tile_pool(name="x_in", bufs=3))
+            k_in = first_phase.enter_context(tc.tile_pool(name="k_in", bufs=3))
+            x_work = first_phase.enter_context(tc.tile_pool(name="x_work", bufs=3))
+            x_mx = first_phase.enter_context(tc.tile_pool(name="x_mx", bufs=5))
+            k_order = first_phase.enter_context(tc.tile_pool(name="k_order", bufs=2))
+            k_work = first_phase.enter_context(tc.tile_pool(name="k_work", bufs=2))
+            x_raw_of, x_grouped_of, x_mx_of, q_grouped_of = {}, {}, {}, {}
+            k_raw_of, k_by_head_of, k_grouped_of = {}, {}, {}
 
-        def load(tile, view, half, col_tile, first=0, last=GROUPS):
-            for t in range(PACK):
-                nc.sync.dma_start(
-                    out=tile[t:P:PACK, first * GROUP_WORK : last * GROUP_WORK].rearrange(
-                        "p (g f) -> p g f", f=GROUP_WORK
-                    ),
-                    in_=view[half, col_tile, t][:, first:last],
-                )
-
-        def load_x(job):
-            x_raw = x_in.tile([P, GROUPS * GROUP_WORK], BF16)
-            x_raw_of[job] = x_raw
-            if job > 0:
-                load(x_raw, x_view, job % HALVES, job // HALVES)
-
-        def turn_x(job, g):
-            x_words = x_raw_of[job][:].bitcast(F32)
-            x_grouped = x_work.tile([P, GROUP_WORK], BF16, align_bytes=64)
-            x_grouped_of[job, g] = x_grouped
-            x_grouped_words = x_grouped[:].bitcast(F32)
-            for bank in range(2):
-                turned = turn_psum.tile([P, 2, 2, P], F32, tag="turn")
-                for s in range(2):
-                    for u in range(2):
-                        first = (g * RUN + 2 * bank + s) * (WIDTH // 2) + u * P
-                        nc.tensor.transpose(
-                            turned[:, s, u, :], x_words[:, first : first + P], ident_f32[:]
-                        )
-                (nc.scalar.copy if 2 * job + g < 2 else nc.vector.tensor_copy)(
-                    out=x_grouped_words[:, bank * BANK : (bank + 1) * BANK].rearrange(
-                        "p (s c u) -> p s c u", s=2, u=2
-                    ),
-                    in_=turned[:].rearrange("p s u c -> p s c u"),
-                )
-
-        def quantise_x(job, g):
-            x_codes = x_work.tile([P, BANK], U32, align_bytes=64)
-            x_scales = x_work.tile([P, BANK], U8, align_bytes=64)
-            x_mx_of[job, g] = (x_codes, x_scales)
-            nc.vector.quantize_mx(
-                out=x_codes[:].bitcast(FP8X4), scales=x_scales[:], in_=x_grouped_of[job, g][:]
-            )
-
-        def project(job, g):
-            x_codes, x_scales = x_mx_of[job, g]
-            q_grouped = x_work.tile([P, PAIRS * BANK], BF16, align_bytes=64)
-            q_grouped_of[job, g] = q_grouped
-            for pair in range(PAIRS):
-                q_acc = acc_psum.tile([P, BANK], F32, tag="acc")
-                nc.tensor.matmul_mx(
-                    out=q_acc[:],
-                    lhsT=w_codes[:, pair * P : (pair + 1) * P].bitcast(FP8X4),
-                    lhsT_scale=w_scales[:, pair * P : (pair + 1) * P],
-                    rhs=x_codes[:].bitcast(FP8X4),
-                    rhs_scale=x_scales[:],
-                    start=True,
-                    stop=True,
-                )
-                nc.scalar.activation(
-                    out=q_grouped[:, pair * BANK : (pair + 1) * BANK].rearrange(
-                        "p (c b t) -> p c b t", b=RUN, t=PACK
-                    ),
-                    in_=q_acc[:].rearrange("p (b c t) -> p c b t", b=RUN, t=PACK),
-                    func=ACT.Identity,
-                    bias=bias[:, pair : pair + 1],
-                    scale=SCALING,
-                )
-
-        def quantise_q(job, g):
-            packed = packed_queries(job, 2 * g)
-            nc.vector.quantize_mx(
-                out=packed[:, 0:BANK].bitcast(FP8X4),
-                scales=packed[:, BANK:SIDE].bitcast(U8),
-                in_=q_grouped_of[job, g][:],
-            )
-
-        def regroup(job, step):
-            even, odd, both = (packed_queries(job, part) for part in range(3))
-            if step == 0:
-                nc.sync.dma_start(out=odd[0:HEAD_DIM, :], in_=even[HEAD_DIM:P, :])
-            elif step == 1:
-                nc.sync.dma_start(out=odd[HEAD_DIM:P, :], in_=both[HEAD_DIM:P, :])
-            else:
-                nc.sync.dma_start(out=even[HEAD_DIM:P, :], in_=both[0:HEAD_DIM, :])
-
-        def attend_scores(n):
-            it, h = n // HEADS, n % HEADS
-            scores = acc_psum.tile([P, COLS], F32, tag="acc")
-            for side, half in ((0, 0), (0, 1), (1, 0), (1, 1)):
-                packed = packed_queries(it * HALVES + half, h % 2)
-                q_first = (h // 2) * P
-                k_first = ((half * 2 + side) * HEADS + h) * KEY_SIDE
-                nc.tensor.matmul_mx(
-                    out=scores[:, side * KEY_SIDE : (side + 1) * KEY_SIDE],
-                    lhsT=packed[:, q_first : q_first + P].bitcast(FP8X4),
-                    lhsT_scale=packed[:, BANK:SIDE].bitcast(U8)[:, q_first : q_first + P],
-                    rhs=k_codes[:, k_first : k_first + KEY_SIDE].bitcast(FP8X4),
-                    rhs_scale=k_scales[:, k_first : k_first + KEY_SIDE],
-                    start=(half == 0),
-                    stop=(half == HALVES - 1),
-                )
-            scores_of[n] = scores
-
-        def attend_max(n):
-            neg_max = soft.tile([P, 1], F32)
-            nc.vector.tensor_reduce(
-                out=neg_max[:], in_=scores_of[n][:], axis=mybir.AxisListType.X, op=ALU.max,
-                negate=True,
-            )
-            scores_of[n] = (scores_of[n], neg_max)
-
-        def attend_exp(n):
-            scores, neg_max = scores_of[n]
-            probs = probs_pool.tile([P, COLS], F32)
-            if n % 2 == 0:
-                total = soft.tile([P, 2], F32)
-                total_of[n // 2] = total
-            nc.scalar.activation(
-                out=probs[:].rearrange("p (tile c b) -> p tile c b", b=RUN, tile=COL_TILES),
-                in_=scores[:].rearrange("p (tile b c) -> p tile c b", b=RUN, tile=COL_TILES),
-                func=ACT.Exp,
-                bias=neg_max[:, 0:1],
-                scale=1.0,
-                accum_out=total_of[n // 2][:, n % 2 : n % 2 + 1],
-            )
-            probs_of[n] = probs
-
-        def attend_inverse(pair):
-            inverse = soft.tile([P, 2], F32)
-            nc.vector.reciprocal(out=inverse[:], in_=total_of[pair][:])
-            total_of[pair] = inverse
-
-        def attend_normalise(pair):
-            inverse = total_of[pair]
-            for n in (2 * pair, 2 * pair + 1):
-                it, h = n // HEADS, n % HEADS
-                probs = probs_of[n]
-                if n % 8 == 7:
-                    nc.scalar.activation(
-                        out=probs[:], in_=probs[:], func=ACT.Copy, scale=inverse[:, n % 2 : n % 2 + 1]
+            def load(tile, view, half, col_tile, first=0, last=GROUPS):
+                for t in range(PACK):
+                    nc.sync.dma_start(
+                        out=tile[t:P:PACK, first * GROUP_WORK : last * GROUP_WORK].rearrange(
+                            "p (g f) -> p g f", f=GROUP_WORK
+                        ),
+                        in_=view[half, col_tile, t][:, first:last],
                     )
-                    continue
-                engine = nc.vector if n % 8 == 3 else nc.gpsimd
-                engine.tensor_scalar(
-                    out=probs[:], in0=probs[:], scalar1=inverse[:, n % 2 : n % 2 + 1], scalar2=0.0,
-                    op0=ALU.mult, op1=ALU.add,
-                )
 
-        def store(n):
-            it, h = n // HEADS, n % HEADS
-            nc.sync.dma_start(out=out_view[:, h, it, :], in_=probs_of[n][:])
-
-        def x_piece(n):
-            return ("x", n // GROUPS, n % GROUPS)
-
-        def key_job(n):
-            return ("k", n, 0)
-
-        items = [x_piece(0), x_piece(1)]
-        for n in range(KEY_JOBS):
-            items.append(key_job(n))
-            for m in range(2 * n + 2, min(2 * n + 4, 2 * X_JOBS)):
-                items.append(x_piece(m))
-        state = {"map": 0}
-
-        def reload_x(tick):
-            freed = item_at(tick - 1, "x")
-            if freed and freed[1] == 1 and freed[0] + 3 < X_JOBS:
-                load_x(freed[0] + 3)
-
-        def item_at(tick, kind):
-            if 0 <= tick < len(items) and items[tick][0] == kind:
-                return items[tick][1:]
-            return None
-
-        def attend(count):
-            for c in range(count):
-                n = state["map"]
-                if n < MAPS:
-                    attend_scores(n)
-                    attend_max(n)
-                if 1 <= n <= MAPS:
-                    attend_exp(n - 1)
-                if 3 <= n <= MAPS + 2 and n % 2 == 1:
-                    attend_inverse((n - 3) // 2)
-                if 4 <= n <= MAPS + 3 and n % 2 == 0:
-                    attend_normalise((n - 4) // 2)
-                if 0 <= n - STORE_LAG < MAPS:
-                    store(n - STORE_LAG)
-                state["map"] = n + 1
-
-        with ExitStack() as key_phase:
-            k_in = key_phase.enter_context(tc.tile_pool(name="k_in", bufs=3))
-            k_order = key_phase.enter_context(tc.tile_pool(name="k_order", bufs=2))
-            k_work = key_phase.enter_context(tc.tile_pool(name="k_work", bufs=1))
+            def load_x(job):
+                x_raw = x_in.tile([P, GROUPS * GROUP_WORK], BF16)
+                x_raw_of[job] = x_raw
+                if job > 0:
+                    load(x_raw, x_view, job % HALVES, job // HALVES)
 
             def load_keys(job):
                 k_raw = k_in.tile([P, GROUPS * GROUP_WORK], BF16)
                 load(k_raw, k_view, job // COL_TILES, job % COL_TILES)
                 k_raw_of[job] = k_raw
+
+            def empty_bank(on_vector, dst, src):
+                if on_vector:
+                    nc.vector.tensor_copy(out=dst, in_=src)
+                else:
+                    nc.scalar.copy(out=dst, in_=src)
+
+            def turn_x(job, g, vector_banks, banks=(0, 1)):
+                x_words = x_raw_of[job][:].bitcast(F32)
+                if banks[0] == 0:
+                    x_grouped = x_work.tile([P, GROUP_WORK], BF16, align_bytes=64)
+                    x_grouped_of[job, g] = x_grouped
+                x_grouped_words = x_grouped_of[job, g][:].bitcast(F32)
+                for bank in banks:
+                    turned = turn_psum.tile([P, 2, 2, P], F32, tag="turn")
+                    for s in range(2):
+                        for u in range(2):
+                            first = (g * RUN + 2 * bank + s) * (WIDTH // 2) + u * P
+                            nc.tensor.transpose(
+                                turned[:, s, u, :], x_words[:, first : first + P], ident_f32[:]
+                            )
+                    empty_bank(
+                        bank in vector_banks,
+                        x_grouped_words[:, bank * BANK : (bank + 1) * BANK].rearrange(
+                            "p (s c u) -> p s c u", s=2, u=2
+                        ),
+                        turned[:].rearrange("p s u c -> p s c u"),
+                    )
+
+            def quantise_x(job, g):
+                x_codes = x_mx.tile([P, BANK], U32, align_bytes=64)
+                x_scales = x_mx.tile([P, BANK], U8, align_bytes=64)
+                x_mx_of[job, g] = (x_codes, x_scales)
+                nc.vector.quantize_mx(
+                    out=x_codes[:].bitcast(FP8X4), scales=x_scales[:], in_=x_grouped_of[job, g][:]
+                )
+
+            def project(job, g, pairs):
+                if pairs[0] == 0:
+                    q_grouped = x_work.tile([P, PAIRS * BANK], BF16, align_bytes=64)
+                    q_grouped_of[job, g] = q_grouped
+                q_grouped = q_grouped_of[job, g]
+                for pair in pairs:
+                    q_acc = acc_psum.tile([P, BANK], F32, tag="acc")
+                    x_codes, x_scales = x_mx_of[job, g]
+                    first = pair * P
+                    nc.tensor.matmul_mx(
+                        out=q_acc[:],
+                        lhsT=w_codes[:, first : first + P].bitcast(FP8X4),
+                        lhsT_scale=w_scales[:, first : first + P],
+                        rhs=x_codes[:].bitcast(FP8X4),
+                        rhs_scale=x_scales[:],
+                        start=True,
+                        stop=True,
+                    )
+                    nc.scalar.activation(
+                        out=q_grouped[:, pair * BANK : (pair + 1) * BANK].rearrange(
+                            "p (c b t) -> p c b t", b=RUN, t=PACK
+                        ),
+                        in_=q_acc[:].rearrange("p (b c t) -> p c b t", b=RUN, t=PACK),
+                        func=ACT.Identity,
+                        bias=bias[:, pair : pair + 1],
+                        scale=SCALING,
+                    )
+
+            def quantise_q(job, g):
+                packed = packed_queries(job, 2 * g)
+                nc.vector.quantize_mx(
+                    out=packed[:, 0:BANK].bitcast(FP8X4),
+                    scales=packed[:, BANK:SIDE].bitcast(U8),
+                    in_=q_grouped_of[job, g][:],
+                )
+
+            def regroup(job, step):
+                even, odd, both = (packed_queries(job, part) for part in range(3))
+                if step == 0:
+                    nc.sync.dma_start(out=odd[0:HEAD_DIM, :], in_=even[HEAD_DIM:P, :])
+                elif step == 1:
+                    nc.sync.dma_start(out=odd[HEAD_DIM:P, :], in_=both[HEAD_DIM:P, :])
+                else:
+                    nc.sync.dma_start(out=even[HEAD_DIM:P, :], in_=both[0:HEAD_DIM, :])
 
             def order_keys(job):
                 k_by_head = k_order.tile([P, GROUPS * GROUP_WORK], BF16)
@@ -279,8 +183,8 @@ def tile_rowselfattention_pa_t_kernel(tc, x, Wq, bq, k, out):
                     in_=k_raw_of[job][:].rearrange("p (g n d) -> p n g d", g=GROUPS, d=HEAD_DIM),
                 )
 
-            def turn_keys(job):
-                if job % 2 == 0:
+            def turn_keys(job, banks):
+                if job % 2 == 0 and banks[0] == 0:
                     k_grouped = k_work.tile([P, 2 * GROUPS * GROUP_WORK], BF16, align_bytes=64)
                     k_grouped_of[job // 2] = k_grouped
                 k_grouped = k_grouped_of[job // 2]
@@ -288,7 +192,7 @@ def tile_rowselfattention_pa_t_kernel(tc, x, Wq, bq, k, out):
                     "p (h n) -> p h n", h=HEADS
                 )[:, :, job % 2 * 256 : (job % 2 + 1) * 256]
                 k_by_head = k_by_head_of[job]
-                for bank in range(4):
+                for bank in banks:
                     turned = turn_psum.tile([P, 8, P], BF16, tag="turn")
                     for s in range(8):
                         h, b = 2 * bank + s // RUN, s % RUN
@@ -320,12 +224,13 @@ def tile_rowselfattention_pa_t_kernel(tc, x, Wq, bq, k, out):
                     out=w_raw[:].rearrange("p (u e) c -> p u (e c)", u=2),
                     in_=Wq.rearrange("(u p e) c -> p u (e c)", u=2, e=2),
                 )
-                bq_rows = setup.tile([P, P], BF16)
-                nc.vector.memset(bq_rows[:], 0.0)
-                load(x_raw_of[0], x_view, 0, 0, 1, 2)
+                bq_pairs = setup.tile([P, P], BF16)
+                nc.vector.memset(bq_pairs[:], 0.0)
                 nc.sync.dma_start(
-                    out=bq_rows[0:PAIRS, :], in_=bq.rearrange("(h d) -> h d", h=PAIRS)
+                    out=bq_pairs[0:PAIRS, :], in_=bq.rearrange("(n f) -> n f", n=PAIRS)
                 )
+                load(x_raw_of[0], x_view, 0, 0, 1, 2)
+                w_grouped = setup.tile([P, WIDTH * PACK], BF16, align_bytes=64)
                 load_keys(0)
                 load_x(1)
                 load_keys(1)
@@ -336,17 +241,20 @@ def tile_rowselfattention_pa_t_kernel(tc, x, Wq, bq, k, out):
                 nc.gpsimd.memset(
                     q_packed[:].rearrange("p (n w) -> p n w", w=SIDE)[:, :, BANK:SIDE], 0
                 )
-                w_grouped = setup.tile([P, WIDTH * PACK], BF16, align_bytes=64)
-                nc.vector.tensor_copy(
-                    out=w_grouped[:].rearrange("p (c t) -> p c t", t=PACK),
-                    in_=w_raw[:].rearrange("p t c -> p c t"),
-                )
-                nc.vector.quantize_mx(
-                    out=w_codes[:].bitcast(FP8X4), scales=w_scales[:], in_=w_grouped[:]
-                )
-                turn_x(0, 0)
+                turn_x(0, 0, (1,))
+                for half in range(2):
+                    cols = slice(half * 256, (half + 1) * 256)
+                    words = slice(half * 1024, (half + 1) * 1024)
+                    empty_bank(
+                        half == 0,
+                        w_grouped[:, words].rearrange("p (c t) -> p c t", t=PACK),
+                        w_raw[:, :, cols].rearrange("p t c -> p c t"),
+                    )
+                    nc.vector.quantize_mx(
+                        out=w_codes[:, cols].bitcast(FP8X4), scales=w_scales[:, cols], in_=w_grouped[:, words]
+                    )
                 bq_turned = acc_psum.tile([P, P], BF16, tag="acc")
-                nc.tensor.transpose(bq_turned[:], bq_rows[:], ident_bf16[:])
+                nc.tensor.transpose(bq_turned[:], bq_pairs[:], ident_bf16[:])
                 nc.vector.tensor_scalar(
                     out=bias[:],
                     in0=bq_turned[:, 0:PAIRS],
@@ -354,50 +262,138 @@ def tile_rowselfattention_pa_t_kernel(tc, x, Wq, bq, k, out):
                     scalar2=None,
                     op0=ALU.mult,
                 )
+                quantise_x(0, 0)
+                turn_x(0, 1, (1,))
+                project(0, 0, range(2))
+                quantise_x(0, 1)
+                order_keys(0)
 
-            ready, half_moved = [], []
-            for tick in range(len(items) + 5):
-                keys, piece = item_at(tick - 1, "k"), item_at(tick - 1, "x")
-                if keys and keys[0] + 3 < KEY_JOBS:
-                    load_keys(keys[0] + 3)
-                if piece and piece[1] == 1 and piece[0] + 3 < X_JOBS:
-                    load_x(piece[0] + 3)
-                if tick >= 2 and item_at(tick + 2, "k"):
-                    order_keys(item_at(tick + 2, "k")[0])
-                if tick == 2:
-                    project(0, 0)
-                if item_at(tick, "k"):
-                    turn_keys(item_at(tick, "k")[0])
-                if tick > 0 and item_at(tick, "x"):
-                    turn_x(*item_at(tick, "x"))
-                if tick > 2 and item_at(tick - 2, "x"):
-                    project(*item_at(tick - 2, "x"))
-                if item_at(tick - 1, "x"):
-                    quantise_x(*item_at(tick - 1, "x"))
-                for part in range(2):
-                    keys = item_at(tick - 1 - part, "k")
-                    if keys and keys[0] % 2 == 1:
-                        quantise_keys(keys[0], part)
-                if tick >= LOADS_DONE:
-                    for job in half_moved:
-                        regroup(job, 2)
-                    for job in ready:
-                        regroup(job, 0)
-                        regroup(job, 1)
-                    half_moved, ready = ready, []
-                piece = item_at(tick - 4, "x")
-                if piece:
-                    quantise_q(*piece)
-                    if piece[1] == 1:
-                        ready.append(piece[0])
-                if tick == 1:
-                    order_keys(0)
-            for job in half_moved:
-                regroup(job, 2)
-            for job in ready:
-                regroup(job, 0)
-                regroup(job, 1)
-                regroup(job, 2)
+            for step in range(X_JOBS):
+                ahead = step + 1
+                first_unit = 1 if step == 0 else 0
+                if step + 3 < KEY_JOBS:
+                    load_keys(step + 3)
+                if step + 3 < X_JOBS:
+                    load_x(step + 3)
+                for group in range(4):
+                    pairs = range(2 * (group % 2), 2 * (group % 2) + 2)
+                    if step == 0 and group > 0:
+                        project(step, group // 2, pairs)
+                    if ahead < X_JOBS:
+                        if group == 0:
+                            turn_x(ahead, 0, XV[0])
+                        elif group < 3:
+                            turn_x(ahead, 1, XV[1], (group - 1,))
+                    if ahead < X_JOBS:
+                        key_banks = ((), (0,), (1,), (2, 3))[group]
+                    else:
+                        key_banks = ((0, 1), (2, 3), (), ())[group]
+                    if key_banks:
+                        turn_keys(step, key_banks)
+                    if step > 0:
+                        project(step, group // 2, pairs)
+                    if group == 0 and step >= 1:
+                        quantise_q(step - 1, 1)
+                    if group == 1:
+                        if ahead < X_JOBS:
+                            quantise_x(ahead, 0)
+                        if step >= 1:
+                            regroup(step - 1, 0)
+                            regroup(step - 1, 1)
+                        if step >= 2:
+                            regroup(step - 2, 2)
+                        if step % 2 == 0 and step >= 2:
+                            quantise_keys(step - 1, 0)
+                    if group == 2:
+                        if step + 1 < KEY_JOBS:
+                            order_keys(step + 1)
+                        quantise_q(step, 0)
+                        if ahead == X_JOBS:
+                            quantise_keys(step, 0)
+                    if group == 3:
+                        if ahead < X_JOBS:
+                            quantise_x(ahead, 1)
+                        if step % 2 == 0 and step >= 2:
+                            quantise_keys(step - 1, 1)
+                        if ahead == X_JOBS:
+                            quantise_keys(step, 1)
+            quantise_q(X_JOBS - 1, 1)
+            regroup(X_JOBS - 2, 2)
+            for step in range(3):
+                regroup(X_JOBS - 1, step)
 
-        probs_pool = ctx.enter_context(tc.tile_pool(name="probs_pool", bufs=16))
-        attend(MAPS + STORE_LAG)
+        probs_pool = ctx.enter_context(tc.tile_pool(name="probs_pool", bufs=12))
+        soft = ctx.enter_context(tc.tile_pool(name="soft", bufs=8))
+        scores_of, probs_of, total_of = {}, {}, {}
+
+        def attend_scores(n):
+            it, h = n // HEADS, n % HEADS
+            scores = acc_psum.tile([P, COLS], F32, tag="acc")
+            for side, half in ((0, 0), (0, 1), (1, 0), (1, 1)):
+                packed = packed_queries(it * HALVES + half, h % 2)
+                q_first = (h // 2) * P
+                k_first = ((half * 2 + side) * HEADS + h) * KEY_SIDE
+                nc.tensor.matmul_mx(
+                    out=scores[:, side * KEY_SIDE : (side + 1) * KEY_SIDE],
+                    lhsT=packed[:, q_first : q_first + P].bitcast(FP8X4),
+                    lhsT_scale=packed[:, BANK:SIDE].bitcast(U8)[:, q_first : q_first + P],
+                    rhs=k_codes[:, k_first : k_first + KEY_SIDE].bitcast(FP8X4),
+                    rhs_scale=k_scales[:, k_first : k_first + KEY_SIDE],
+                    start=(half == 0),
+                    stop=(half == HALVES - 1),
+                )
+            neg_max = soft.tile([P, 1], F32)
+            nc.vector.tensor_reduce(
+                out=neg_max[:], in_=scores[:], axis=mybir.AxisListType.X, op=ALU.max, negate=True
+            )
+            scores_of[n] = (scores, neg_max)
+
+        def attend_exp(n):
+            scores, neg_max = scores_of[n]
+            probs = probs_pool.tile([P, COLS], F32)
+            if n % 2 == 0:
+                total = soft.tile([P, 2], F32)
+                total_of[n // 2] = total
+            nc.scalar.activation(
+                out=probs[:].rearrange("p (tile c b) -> p tile c b", b=RUN, tile=COL_TILES),
+                in_=scores[:].rearrange("p (tile b c) -> p tile c b", b=RUN, tile=COL_TILES),
+                func=ACT.Exp,
+                bias=neg_max[:, 0:1],
+                scale=1.0,
+                accum_out=total_of[n // 2][:, n % 2 : n % 2 + 1],
+            )
+            probs_of[n] = probs
+
+        def attend_inverse(pair):
+            inverse = soft.tile([P, 2], F32)
+            nc.vector.reciprocal(out=inverse[:], in_=total_of[pair][:])
+            total_of[pair] = inverse
+
+        def attend_normalise(pair):
+            inverse = total_of[pair]
+            for n in (2 * pair, 2 * pair + 1):
+                probs, factor = probs_of[n], inverse[:, n % 2 : n % 2 + 1]
+                if n % 8 == 7:
+                    nc.scalar.activation(out=probs[:], in_=probs[:], func=ACT.Copy, scale=factor)
+                else:
+                    engine = nc.gpsimd
+                    engine.tensor_scalar(
+                        out=probs[:], in0=probs[:], scalar1=factor, scalar2=0.0,
+                        op0=ALU.mult, op1=ALU.add,
+                    )
+
+        def attend_store(n):
+            it, h = n // HEADS, n % HEADS
+            nc.sync.dma_start(out=out_view[:, h, it, :], in_=probs_of[n][:])
+
+        for n in range(MAPS + STORE_LAG):
+            if n < MAPS:
+                attend_scores(n)
+            if 1 <= n <= MAPS:
+                attend_exp(n - 1)
+            if 3 <= n <= MAPS + 2 and n % 2 == 1:
+                attend_inverse((n - 3) // 2)
+            if 4 <= n <= MAPS + 3 and n % 2 == 0:
+                attend_normalise((n - 4) // 2)
+            if n >= STORE_LAG:
+                attend_store(n - STORE_LAG)

@@ -30,6 +30,9 @@ X_JOBS = COL_TILES * HALVES
 KEY_JOBS = COL_TILES * HALVES
 STORE_LAG = 6
 STAGES = 4
+WARM = 1
+UNITS = ((0, 1, 2), (3, 4, 5), (6, 7))
+FIRST_UNITS = ((2, 3), (4, 5), (6, 7))
 XV = ((0, 1), (0, 1))
 
 FLOPS = 2 * ROWS * COLS * WIDTH * WIDTH + 2 * HEADS * COLS * COLS * ROWS * HEAD_DIM
@@ -53,6 +56,8 @@ def tile_rowselfattention_pa_t_kernel(tc, x, Wq, bq, k, out):
 
         ident_f32 = keep.tile([P, P], F32)
         ident_bf16 = keep.tile([P, P], BF16)
+        zeros = keep.tile([P, BANK], BF16)
+        nc.vector.memset(zeros[:], 0.0)
         w_codes = keep.tile([P, WIDTH], U32, align_bytes=64)
         w_scales = keep.tile([P, WIDTH], U8, align_bytes=64)
         bias = keep.tile([P, PAIRS], F32)
@@ -130,13 +135,19 @@ def tile_rowselfattention_pa_t_kernel(tc, x, Wq, bq, k, out):
                     out=x_codes[:].bitcast(FP8X4), scales=x_scales[:], in_=x_grouped_of[job, g][:]
                 )
 
-            def project(job, g, pairs):
-                if pairs[0] == 0:
-                    q_grouped = x_work.tile([P, PAIRS * BANK], BF16, align_bytes=64)
-                    q_grouped_of[job, g] = q_grouped
-                q_grouped = q_grouped_of[job, g]
-                for pair in pairs:
+            def keep_warm(bank):
+                nc.tensor.matmul(bank[:], lhsT=zeros[:, 0:P], rhs=zeros[:], start=True, stop=True)
+
+            def project(job, units):
+                for n, unit in enumerate(units):
+                    g, pair = unit // PAIRS, unit % PAIRS
+                    if pair == 0:
+                        q_grouped = x_work.tile([P, PAIRS * BANK], BF16, align_bytes=64)
+                        q_grouped_of[job, g] = q_grouped
+                    q_grouped = q_grouped_of[job, g]
                     q_acc = acc_psum.tile([P, BANK], F32, tag="acc")
+                    if n < WARM:
+                        keep_warm(q_acc)
                     x_codes, x_scales = x_mx_of[job, g]
                     first = pair * P
                     nc.tensor.matmul_mx(
@@ -264,7 +275,7 @@ def tile_rowselfattention_pa_t_kernel(tc, x, Wq, bq, k, out):
                 )
                 quantise_x(0, 0)
                 turn_x(0, 1, (1,))
-                project(0, 0, range(2))
+                project(0, (0, 1))
                 quantise_x(0, 1)
                 order_keys(0)
 
@@ -275,42 +286,42 @@ def tile_rowselfattention_pa_t_kernel(tc, x, Wq, bq, k, out):
                     load_keys(step + 3)
                 if step + 3 < X_JOBS:
                     load_x(step + 3)
-                for group in range(4):
-                    pairs = range(2 * (group % 2), 2 * (group % 2) + 2)
-                    if step == 0 and group > 0:
-                        project(step, group // 2, pairs)
+                for group in range(3):
+                    units = UNITS[group] if step > 0 else FIRST_UNITS[group]
+                    if step == 0:
+                        project(step, units)
                     if ahead < X_JOBS:
                         if group == 0:
-                            turn_x(ahead, 0, XV[0])
-                        elif group < 3:
-                            turn_x(ahead, 1, XV[1], (group - 1,))
-                    if ahead < X_JOBS:
-                        key_banks = ((), (0,), (1,), (2, 3))[group]
+                            turn_x(ahead, 0, (0, 1))
+                            turn_x(ahead, 1, (0, 1), (0,))
+                        elif group == 1:
+                            turn_x(ahead, 1, (0, 1), (1,))
+                        key_banks = ((), (0, 1), (2, 3))[group]
                     else:
-                        key_banks = ((0, 1), (2, 3), (), ())[group]
+                        key_banks = ((0, 1, 2), (3,), ())[group]
                     if key_banks:
                         turn_keys(step, key_banks)
                     if step > 0:
-                        project(step, group // 2, pairs)
-                    if group == 0 and step >= 1:
-                        quantise_q(step - 1, 1)
-                    if group == 1:
-                        if ahead < X_JOBS:
-                            quantise_x(ahead, 0)
+                        project(step, units)
+                    if group == 0:
                         if step >= 1:
+                            quantise_q(step - 1, 1)
                             regroup(step - 1, 0)
-                            regroup(step - 1, 1)
                         if step >= 2:
                             regroup(step - 2, 2)
+                        if ahead < X_JOBS:
+                            quantise_x(ahead, 0)
                         if step % 2 == 0 and step >= 2:
                             quantise_keys(step - 1, 0)
-                    if group == 2:
+                    if group == 1:
+                        if step >= 1:
+                            regroup(step - 1, 1)
                         if step + 1 < KEY_JOBS:
                             order_keys(step + 1)
-                        quantise_q(step, 0)
                         if ahead == X_JOBS:
                             quantise_keys(step, 0)
-                    if group == 3:
+                    if group == 2:
+                        quantise_q(step, 0)
                         if ahead < X_JOBS:
                             quantise_x(ahead, 1)
                         if step % 2 == 0 and step >= 2:

@@ -19,6 +19,7 @@ ROWS, COLS, WIDTH, HEADS, HEAD_DIM = 16, 512, 512, 8, 64
 RUN = 4
 COL_TILES = COLS // P
 HALVES = 2
+HALF_ROWS = 8
 GROUPS = 2
 PAIRS = HEADS // 2
 SCALING = 1.0 / 32.0
@@ -29,7 +30,7 @@ MAPS = COL_TILES * HEADS
 X_JOBS = COL_TILES * HALVES
 KEY_JOBS = COL_TILES * HALVES
 STORE_LAG = 6
-STAGES = 4
+LOADS_DONE = 5
 WARM = 1
 UNITS = ((0, 1, 2), (3, 4, 5), (6, 7))
 FIRST_UNITS = ((2, 3), (4, 5), (6, 7))
@@ -40,9 +41,7 @@ FLOPS = 2 * ROWS * COLS * WIDTH * WIDTH + 2 * HEADS * COLS * COLS * ROWS * HEAD_
 
 def tile_rowselfattention_pa_t_kernel(tc, x, Wq, bq, k, out):
     nc = tc.nc
-    x_view = x[:, :, 0, :].rearrange(
-        "(half g t) (tile c b) e -> half tile t c g (b e)", half=HALVES, g=GROUPS, tile=COL_TILES, b=RUN
-    )
+    x_view = x[:, :, 0, :].rearrange("r (t p) e -> p t r e", p=P)
     k_view = k[:, :, 0].rearrange(
         "(half g t) (tile c b) h d -> half tile t c g (b h d)", half=HALVES, g=GROUPS, tile=COL_TILES, b=RUN
     )
@@ -63,41 +62,46 @@ def tile_rowselfattention_pa_t_kernel(tc, x, Wq, bq, k, out):
         bias = keep.tile([P, PAIRS], F32)
         k_codes = keep.tile([P, HEADS * HALVES * COLS], U32, align_bytes=64)
         k_scales = keep.tile([P, HEADS * HALVES * COLS], U8, align_bytes=64)
-        q_packed = keep.tile([P, (2 * X_JOBS + STAGES) * SIDE], I32, align_bytes=64)
+        q_packed = keep.tile([P, 3 * X_JOBS * SIDE], I32, align_bytes=64)
 
         def packed_queries(job, part):
-            n = 2 * job + part if part < 2 else 2 * X_JOBS + job % STAGES
+            n = 3 * job + part
             return q_packed[:, n * SIDE : (n + 1) * SIDE]
 
         with ExitStack() as first_phase:
             x_in = first_phase.enter_context(tc.tile_pool(name="x_in", bufs=3))
             k_in = first_phase.enter_context(tc.tile_pool(name="k_in", bufs=3))
-            x_work = first_phase.enter_context(tc.tile_pool(name="x_work", bufs=3))
-            x_mx = first_phase.enter_context(tc.tile_pool(name="x_mx", bufs=5))
+            x_work = first_phase.enter_context(tc.tile_pool(name="x_work", bufs=2))
+            x_mx = first_phase.enter_context(tc.tile_pool(name="x_mx", bufs=4))
             k_order = first_phase.enter_context(tc.tile_pool(name="k_order", bufs=2))
             k_work = first_phase.enter_context(tc.tile_pool(name="k_work", bufs=2))
             x_raw_of, x_grouped_of, x_mx_of, q_grouped_of = {}, {}, {}, {}
             k_raw_of, k_by_head_of, k_grouped_of = {}, {}, {}
 
-            def load(tile, view, half, col_tile, first=0, last=GROUPS):
-                for t in range(PACK):
-                    nc.sync.dma_start(
-                        out=tile[t:P:PACK, first * GROUP_WORK : last * GROUP_WORK].rearrange(
-                            "p (g f) -> p g f", f=GROUP_WORK
-                        ),
-                        in_=view[half, col_tile, t][:, first:last],
-                    )
+            def load_rows(x_raw, job, first, count):
+                it, half = job // HALVES, job % HALVES
+                row = half * HALF_ROWS + first
+                nc.sync.dma_start(
+                    out=x_raw[:, first * WIDTH : (first + count) * WIDTH].rearrange(
+                        "p (r e) -> p r e", r=count
+                    ),
+                    in_=x_view[:, it, row : row + count, :],
+                )
 
             def load_x(job):
-                x_raw = x_in.tile([P, GROUPS * GROUP_WORK], BF16)
+                x_raw = x_in.tile([P, HALF_ROWS * WIDTH], BF16)
                 x_raw_of[job] = x_raw
                 if job > 0:
-                    load(x_raw, x_view, job % HALVES, job // HALVES)
+                    load_rows(x_raw, job, 0, HALF_ROWS)
 
             def load_keys(job):
                 k_raw = k_in.tile([P, GROUPS * GROUP_WORK], BF16)
-                load(k_raw, k_view, job // COL_TILES, job % COL_TILES)
                 k_raw_of[job] = k_raw
+                for t in range(PACK):
+                    nc.sync.dma_start(
+                        out=k_raw[t:P:PACK, :].rearrange("p (g f) -> p g f", g=GROUPS),
+                        in_=k_view[job // COL_TILES, job % COL_TILES, t],
+                    )
 
             def empty_bank(on_vector, dst, src):
                 if on_vector:
@@ -161,9 +165,9 @@ def tile_rowselfattention_pa_t_kernel(tc, x, Wq, bq, k, out):
                     )
                     nc.scalar.activation(
                         out=q_grouped[:, pair * BANK : (pair + 1) * BANK].rearrange(
-                            "p (c b t) -> p c b t", b=RUN, t=PACK
+                            "p (i t) -> p i t", t=PACK
                         ),
-                        in_=q_acc[:].rearrange("p (b c t) -> p c b t", b=RUN, t=PACK),
+                        in_=q_acc[:].rearrange("p (t i) -> p i t", t=PACK),
                         func=ACT.Identity,
                         bias=bias[:, pair : pair + 1],
                         scale=SCALING,
@@ -229,7 +233,7 @@ def tile_rowselfattention_pa_t_kernel(tc, x, Wq, bq, k, out):
 
             with tc.tile_pool(name="setup", bufs=1) as setup:
                 load_x(0)
-                load(x_raw_of[0], x_view, 0, 0, 0, 1)
+                load_rows(x_raw_of[0], 0, 0, 4)
                 w_raw = setup.tile([P, PACK, WIDTH], BF16)
                 nc.sync.dma_start(
                     out=w_raw[:].rearrange("p (u e) c -> p u (e c)", u=2),
@@ -240,7 +244,7 @@ def tile_rowselfattention_pa_t_kernel(tc, x, Wq, bq, k, out):
                 nc.sync.dma_start(
                     out=bq_pairs[0:PAIRS, :], in_=bq.rearrange("(n f) -> n f", n=PAIRS)
                 )
-                load(x_raw_of[0], x_view, 0, 0, 1, 2)
+                load_rows(x_raw_of[0], 0, 4, 4)
                 w_grouped = setup.tile([P, WIDTH * PACK], BF16, align_bytes=64)
                 load_keys(0)
                 load_x(1)
@@ -282,10 +286,17 @@ def tile_rowselfattention_pa_t_kernel(tc, x, Wq, bq, k, out):
             for step in range(X_JOBS):
                 ahead = step + 1
                 first_unit = 1 if step == 0 else 0
-                if step + 3 < KEY_JOBS:
-                    load_keys(step + 3)
                 if step + 3 < X_JOBS:
                     load_x(step + 3)
+                if step + 3 < KEY_JOBS:
+                    load_keys(step + 3)
+                if step >= LOADS_DONE:
+                    first = 0 if step == LOADS_DONE else step - 2
+                    for job in range(first, step - 1):
+                        regroup(job, 0)
+                        regroup(job, 1)
+                    for job in range(first, step - 1):
+                        regroup(job, 2)
                 for group in range(3):
                     units = UNITS[group] if step > 0 else FIRST_UNITS[group]
                     if step == 0:
@@ -306,16 +317,11 @@ def tile_rowselfattention_pa_t_kernel(tc, x, Wq, bq, k, out):
                     if group == 0:
                         if step >= 1:
                             quantise_q(step - 1, 1)
-                            regroup(step - 1, 0)
-                        if step >= 2:
-                            regroup(step - 2, 2)
                         if ahead < X_JOBS:
                             quantise_x(ahead, 0)
                         if step % 2 == 0 and step >= 2:
                             quantise_keys(step - 1, 0)
                     if group == 1:
-                        if step >= 1:
-                            regroup(step - 1, 1)
                         if step + 1 < KEY_JOBS:
                             order_keys(step + 1)
                         if ahead == X_JOBS:
@@ -329,9 +335,9 @@ def tile_rowselfattention_pa_t_kernel(tc, x, Wq, bq, k, out):
                         if ahead == X_JOBS:
                             quantise_keys(step, 1)
             quantise_q(X_JOBS - 1, 1)
-            regroup(X_JOBS - 2, 2)
-            for step in range(3):
-                regroup(X_JOBS - 1, step)
+            for move in range(3):
+                for job in range(X_JOBS - 2, X_JOBS):
+                    regroup(job, move)
 
         probs_pool = ctx.enter_context(tc.tile_pool(name="probs_pool", bufs=12))
         soft = ctx.enter_context(tc.tile_pool(name="soft", bufs=8))

@@ -32,6 +32,8 @@ KEY_JOBS = COL_TILES * HALVES
 STORE_LAG = 6
 LOADS_DONE = 5
 WARM = 1
+SOLO_STEP = 4
+SOLO = (7,)
 UNITS = ((0, 1, 2), (3, 4, 5), (6, 7))
 FIRST_UNITS = ((2, 3), (4, 5), (6, 7))
 XV = ((0, 1), (0, 1))
@@ -59,14 +61,19 @@ def tile_rowselfattention_pa_t_kernel(tc, x, Wq, bq, k, out):
         nc.vector.memset(zeros[:], 0.0)
         w_codes = keep.tile([P, WIDTH], U32, align_bytes=64)
         w_scales = keep.tile([P, WIDTH], U8, align_bytes=64)
-        bias = keep.tile([P, PAIRS], F32)
+        bias = keep.tile([P, PAIRS + HEADS], F32)
+        bq_heads = keep.tile([P, P], BF16)
         k_codes = keep.tile([P, HEADS * HALVES * COLS], U32, align_bytes=64)
         k_scales = keep.tile([P, HEADS * HALVES * COLS], U8, align_bytes=64)
         q_packed = keep.tile([P, 3 * X_JOBS * SIDE], I32, align_bytes=64)
 
-        def packed_queries(job, part):
-            n = 3 * job + part
-            return q_packed[:, n * SIDE : (n + 1) * SIDE]
+        def query_codes(it, part, halves):
+            first = (3 * it + part) * 2 * SIDE
+            return q_packed[:, first + halves.start * BANK : first + halves.stop * BANK]
+
+        def query_scales(it, part, halves):
+            first = (3 * it + part) * 2 * SIDE + 2 * BANK
+            return q_packed[:, first + halves.start * P : first + halves.stop * P]
 
         with ExitStack() as first_phase:
             x_in = first_phase.enter_context(tc.tile_pool(name="x_in", bufs=3))
@@ -142,6 +149,40 @@ def tile_rowselfattention_pa_t_kernel(tc, x, Wq, bq, k, out):
             def keep_warm(bank):
                 nc.tensor.matmul(bank[:], lhsT=zeros[:, 0:P], rhs=zeros[:], start=True, stop=True)
 
+            def pass_mx(q_acc, codes, scales, first, job, g, start, stop):
+                x_codes, x_scales = x_mx_of[job, g]
+                nc.tensor.matmul_mx(
+                    out=q_acc[:],
+                    lhsT=codes[:, first : first + P].bitcast(FP8X4),
+                    lhsT_scale=scales[:, first : first + P],
+                    rhs=x_codes[:].bitcast(FP8X4),
+                    rhs_scale=x_scales[:],
+                    start=start,
+                    stop=stop,
+                )
+
+            def turn_bias(rows, first, count):
+                bq_turned = acc_psum.tile([P, P], BF16, tag="acc")
+                nc.tensor.transpose(bq_turned[:], rows[:], ident_bf16[:])
+                nc.vector.tensor_scalar(
+                    out=bias[:, first : first + count],
+                    in0=bq_turned[:, 0:count],
+                    scalar1=SCALING,
+                    scalar2=None,
+                    op0=ALU.mult,
+                )
+
+            def prepare_solo():
+                for mixed, plain, width in (
+                    (solo_codes[:].bitcast(I32), w_codes[:].bitcast(I32), HEAD_DIM),
+                    (solo_scales[:].bitcast(I32), w_scales[:].bitcast(I32), HEAD_DIM // PACK),
+                ):
+                    nc.vector.tensor_copy(
+                        out=mixed[:, 0 : 2 * HEADS * width].rearrange("p (h s w) -> p s h w", s=2, w=width)[:, 1],
+                        in_=plain.rearrange("p (h w) -> p h w", w=width),
+                    )
+                turn_bias(bq_heads, PAIRS, HEADS)
+
             def project(job, units):
                 for n, unit in enumerate(units):
                     g, pair = unit // PAIRS, unit % PAIRS
@@ -150,45 +191,47 @@ def tile_rowselfattention_pa_t_kernel(tc, x, Wq, bq, k, out):
                         q_grouped_of[job, g] = q_grouped
                     q_grouped = q_grouped_of[job, g]
                     q_acc = acc_psum.tile([P, BANK], F32, tag="acc")
-                    if n < WARM:
-                        keep_warm(q_acc)
-                    x_codes, x_scales = x_mx_of[job, g]
-                    first = pair * P
-                    nc.tensor.matmul_mx(
-                        out=q_acc[:],
-                        lhsT=w_codes[:, first : first + P].bitcast(FP8X4),
-                        lhsT_scale=w_scales[:, first : first + P],
-                        rhs=x_codes[:].bitcast(FP8X4),
-                        rhs_scale=x_scales[:],
-                        start=True,
-                        stop=True,
-                    )
+                    if job in SOLO:
+                        h = 2 * pair + g
+                        pass_mx(q_acc, solo_codes, solo_scales, (2 * h + 1) * HEAD_DIM, job, 0, True, False)
+                        pass_mx(q_acc, solo_codes, solo_scales, 2 * h * HEAD_DIM, job, 1, False, True)
+                        column = PAIRS + h
+                    else:
+                        if n < WARM:
+                            keep_warm(q_acc)
+                        pass_mx(q_acc, w_codes, w_scales, pair * P, job, g, True, True)
+                        column = pair
                     nc.scalar.activation(
                         out=q_grouped[:, pair * BANK : (pair + 1) * BANK].rearrange(
                             "p (i t) -> p i t", t=PACK
                         ),
                         in_=q_acc[:].rearrange("p (t i) -> p i t", t=PACK),
                         func=ACT.Identity,
-                        bias=bias[:, pair : pair + 1],
+                        bias=bias[:, column : column + 1],
                         scale=SCALING,
                     )
 
             def quantise_q(job, g):
-                packed = packed_queries(job, 2 * g)
+                it, half = job // HALVES, job % HALVES
+                part = g if job in SOLO else 2 * g
                 nc.vector.quantize_mx(
-                    out=packed[:, 0:BANK].bitcast(FP8X4),
-                    scales=packed[:, BANK:SIDE].bitcast(U8),
+                    out=query_codes(it, part, range(half, half + 1)).bitcast(FP8X4),
+                    scales=query_scales(it, part, range(half, half + 1)).bitcast(U8),
                     in_=q_grouped_of[job, g][:],
                 )
 
-            def regroup(job, step):
-                even, odd, both = (packed_queries(job, part) for part in range(3))
-                if step == 0:
-                    nc.sync.dma_start(out=odd[0:HEAD_DIM, :], in_=even[HEAD_DIM:P, :])
-                elif step == 1:
-                    nc.sync.dma_start(out=odd[HEAD_DIM:P, :], in_=both[HEAD_DIM:P, :])
-                else:
-                    nc.sync.dma_start(out=even[HEAD_DIM:P, :], in_=both[0:HEAD_DIM, :])
+            def regroup(its, moves):
+                for move in moves:
+                    for it in its:
+                        halves = range(sum(it * HALVES + half not in SOLO for half in range(HALVES)))
+                        for words in (query_codes, query_scales):
+                            even, odd, both = (words(it, part, halves) for part in range(3))
+                            if move == 0:
+                                nc.sync.dma_start(out=odd[0:HEAD_DIM, :], in_=even[HEAD_DIM:P, :])
+                            elif move == 1:
+                                nc.sync.dma_start(out=odd[HEAD_DIM:P, :], in_=both[HEAD_DIM:P, :])
+                            else:
+                                nc.sync.dma_start(out=even[HEAD_DIM:P, :], in_=both[0:HEAD_DIM, :])
 
             def order_keys(job):
                 k_by_head = k_order.tile([P, GROUPS * GROUP_WORK], BF16)
@@ -251,10 +294,16 @@ def tile_rowselfattention_pa_t_kernel(tc, x, Wq, bq, k, out):
                 load_keys(1)
                 load_x(2)
                 load_keys(2)
+                nc.gpsimd.memset(bq_heads[:], 0.0)
+                for half in range(2):
+                    nc.sync.dma_start(
+                        out=bq_heads[0:HEADS, half * HEAD_DIM : (half + 1) * HEAD_DIM],
+                        in_=bq.rearrange("(h d) -> h d", h=HEADS),
+                    )
                 make_identity(nc, ident_f32[:])
                 make_identity(nc, ident_bf16[:])
                 nc.gpsimd.memset(
-                    q_packed[:].rearrange("p (n w) -> p n w", w=SIDE)[:, :, BANK:SIDE], 0
+                    q_packed[:].rearrange("p (n w) -> p n w", w=2 * SIDE)[:, :, 2 * BANK :], 0
                 )
                 turn_x(0, 0, (1,))
                 for half in range(2):
@@ -268,21 +317,16 @@ def tile_rowselfattention_pa_t_kernel(tc, x, Wq, bq, k, out):
                     nc.vector.quantize_mx(
                         out=w_codes[:, cols].bitcast(FP8X4), scales=w_scales[:, cols], in_=w_grouped[:, words]
                     )
-                bq_turned = acc_psum.tile([P, P], BF16, tag="acc")
-                nc.tensor.transpose(bq_turned[:], bq_pairs[:], ident_bf16[:])
-                nc.vector.tensor_scalar(
-                    out=bias[:],
-                    in0=bq_turned[:, 0:PAIRS],
-                    scalar1=SCALING,
-                    scalar2=None,
-                    op0=ALU.mult,
-                )
+                turn_bias(bq_pairs, 0, PAIRS)
                 quantise_x(0, 0)
                 turn_x(0, 1, (1,))
                 project(0, (0, 1))
                 quantise_x(0, 1)
                 order_keys(0)
 
+            solo = first_phase.enter_context(tc.tile_pool(name="solo", bufs=1))
+            solo_codes = solo.tile([P, (2 * HEADS + 1) * HEAD_DIM], U32, align_bytes=64)
+            solo_scales = solo.tile([P, (2 * HEADS + 1) * HEAD_DIM], U8, align_bytes=64)
             for step in range(X_JOBS):
                 ahead = step + 1
                 first_unit = 1 if step == 0 else 0
@@ -290,13 +334,15 @@ def tile_rowselfattention_pa_t_kernel(tc, x, Wq, bq, k, out):
                     load_x(step + 3)
                 if step + 3 < KEY_JOBS:
                     load_keys(step + 3)
-                if step >= LOADS_DONE:
-                    first = 0 if step == LOADS_DONE else step - 2
-                    for job in range(first, step - 1):
-                        regroup(job, 0)
-                        regroup(job, 1)
-                    for job in range(first, step - 1):
-                        regroup(job, 2)
+                if step == LOADS_DONE:
+                    regroup(range(0, 2), range(3))
+                if step == X_JOBS - 1:
+                    regroup(range(2, 3), range(3))
+                if step == 1:
+                    nc.gpsimd.memset(solo_codes[:].bitcast(I32), 0)
+                    nc.gpsimd.memset(solo_scales[:].bitcast(I32), 0)
+                if step == SOLO_STEP:
+                    prepare_solo()
                 for group in range(3):
                     units = UNITS[group] if step > 0 else FIRST_UNITS[group]
                     if step == 0:
@@ -335,9 +381,7 @@ def tile_rowselfattention_pa_t_kernel(tc, x, Wq, bq, k, out):
                         if ahead == X_JOBS:
                             quantise_keys(step, 1)
             quantise_q(X_JOBS - 1, 1)
-            for move in range(3):
-                for job in range(X_JOBS - 2, X_JOBS):
-                    regroup(job, move)
+            regroup(range(3, 4), range(3))
 
         probs_pool = ctx.enter_context(tc.tile_pool(name="probs_pool", bufs=12))
         soft = ctx.enter_context(tc.tile_pool(name="soft", bufs=8))
@@ -347,13 +391,14 @@ def tile_rowselfattention_pa_t_kernel(tc, x, Wq, bq, k, out):
             it, h = n // HEADS, n % HEADS
             scores = acc_psum.tile([P, COLS], F32, tag="acc")
             for side, half in ((0, 0), (0, 1), (1, 0), (1, 1)):
-                packed = packed_queries(it * HALVES + half, h % 2)
+                q_codes = query_codes(it, h % 2, range(half, half + 1))
+                q_scales = query_scales(it, h % 2, range(half, half + 1)).bitcast(U8)
                 q_first = (h // 2) * P
                 k_first = ((half * 2 + side) * HEADS + h) * KEY_SIDE
                 nc.tensor.matmul_mx(
                     out=scores[:, side * KEY_SIDE : (side + 1) * KEY_SIDE],
-                    lhsT=packed[:, q_first : q_first + P].bitcast(FP8X4),
-                    lhsT_scale=packed[:, BANK:SIDE].bitcast(U8)[:, q_first : q_first + P],
+                    lhsT=q_codes[:, q_first : q_first + P].bitcast(FP8X4),
+                    lhsT_scale=q_scales[:, q_first : q_first + P],
                     rhs=k_codes[:, k_first : k_first + KEY_SIDE].bitcast(FP8X4),
                     rhs_scale=k_scales[:, k_first : k_first + KEY_SIDE],
                     start=(half == 0),

from contextlib import ExitStack

import concourse.mybir as mybir
from concourse.masks import make_identity

F32 = mybir.dt.float32
BF16 = mybir.dt.bfloat16
U32 = mybir.dt.uint32
U8 = mybir.dt.uint8
I32 = mybir.dt.int32
FP8X4 = mybir.dt.float8_e4m3fn_x4
ACT = mybir.ActivationFunctionType
ALU = mybir.AluOpType

P = 128
PACK = 4
BANK = 512
ROWS, COLS, WIDTH, HEADS, HEAD_DIM = 16, 512, 512, 8, 64
RUN = 4
COL_TILES = COLS // P
HALVES = 2
HALF_ROWS = 8
GROUPS = 2
PAIRS = HEADS // 2
SCALING = 1.0 / 32.0
GROUP_WORK = RUN * WIDTH
SIDE = BANK + BANK // 4
KEY_SIDE = 2 * P
MAPS = COL_TILES * HEADS
X_JOBS = COL_TILES * HALVES
KEY_JOBS = COL_TILES * HALVES
STORE_LAG = 6
LOADS_DONE = 5
WARM = 1
SOLO_STEP = 4
SOLO = (7,)
UNITS = ((0, 1, 2), (3, 4, 5), (6, 7))
FIRST_UNITS = ((2, 3), (4, 5), (6, 7))
XV = ((0, 1), (0, 1))

FLOPS = 2 * ROWS * COLS * WIDTH * WIDTH + 2 * HEADS * COLS * COLS * ROWS * HEAD_DIM


def tile_rowselfattention_pa_t_kernel(tc, x, Wq, bq, k, out):
    nc = tc.nc
    x_view = x[:, :, 0, :].rearrange("r (t p) e -> p t r e", p=P)
    k_view = k[:, :, 0].rearrange(
        "(half g t) (tile c b) h d -> half tile t c g (b h d)", half=HALVES, g=GROUPS, tile=COL_TILES, b=RUN
    )
    out_view = out[:, 0].rearrange("h (t p) j -> p h t j", p=P)

    with ExitStack() as ctx:
        ctx.enter_context(tc.manual_schedule())
        keep = ctx.enter_context(tc.tile_pool(name="keep", bufs=1))
        turn_psum = ctx.enter_context(tc.psum_pool(name="turn_psum", bufs=4))
        acc_psum = ctx.enter_context(tc.psum_pool(name="acc_psum", bufs=4))

        ident_f32 = keep.tile([P, P], F32)
        ident_bf16 = keep.tile([P, P], BF16)
        zeros = keep.tile([P, BANK], BF16)
        nc.vector.memset(zeros[:], 0.0)
        w_codes = keep.tile([P, WIDTH], U32, align_bytes=64)
        w_scales = keep.tile([P, WIDTH], U8, align_bytes=64)
        bias = keep.tile([P, PAIRS + HEADS], F32)
        bq_heads = keep.tile([P, P], BF16)
        k_codes = keep.tile([P, HEADS * HALVES * COLS], U32, align_bytes=64)
        k_scales = keep.tile([P, HEADS * HALVES * COLS], U8, align_bytes=64)
        q_packed = keep.tile([P, 3 * X_JOBS * SIDE], I32, align_bytes=64)

        def query_codes(it, part, halves):
            first = (3 * it + part) * 2 * SIDE
            return q_packed[:, first + halves.start * BANK : first + halves.stop * BANK]

        def query_scales(it, part, halves):
            first = (3 * it + part) * 2 * SIDE + 2 * BANK
            return q_packed[:, first + halves.start * P : first + halves.stop * P]

        with ExitStack() as first_phase:
            x_in = first_phase.enter_context(tc.tile_pool(name="x_in", bufs=3))
            k_in = first_phase.enter_context(tc.tile_pool(name="k_in", bufs=3))
            x_work = first_phase.enter_context(tc.tile_pool(name="x_work", bufs=2))
            x_mx = first_phase.enter_context(tc.tile_pool(name="x_mx", bufs=4))
            k_order = first_phase.enter_context(tc.tile_pool(name="k_order", bufs=2))
            k_work = first_phase.enter_context(tc.tile_pool(name="k_work", bufs=2))
            x_raw_of, x_grouped_of, x_mx_of, q_grouped_of = {}, {}, {}, {}
            k_raw_of, k_by_head_of, k_grouped_of = {}, {}, {}

            def load_rows(x_raw, job, first, count):
                it, half = job // HALVES, job % HALVES
                row = half * HALF_ROWS + first
                nc.sync.dma_start(
                    out=x_raw[:, first * WIDTH : (first + count) * WIDTH].rearrange(
                        "p (r e) -> p r e", r=count
                    ),
                    in_=x_view[:, it, row : row + count, :],
                )

            def load_x(job):
                x_raw = x_in.tile([P, HALF_ROWS * WIDTH], BF16)
                x_raw_of[job] = x_raw
                if job > 0:
                    load_rows(x_raw, job, 0, HALF_ROWS)

            def load_keys(job):
                k_raw = k_in.tile([P, GROUPS * GROUP_WORK], BF16)
                k_raw_of[job] = k_raw
                for t in range(PACK):
                    nc.sync.dma_start(
                        out=k_raw[t:P:PACK, :].rearrange("p (g f) -> p g f", g=GROUPS),
                        in_=k_view[job // COL_TILES, job % COL_TILES, t],
                    )

            def empty_bank(on_vector, dst, src):
                if on_vector:
                    nc.vector.tensor_copy(out=dst, in_=src)
                else:
                    nc.scalar.copy(out=dst, in_=src)

            def turn_x(job, g, vector_banks, banks=(0, 1)):
                x_words = x_raw_of[job][:].bitcast(F32)
                if banks[0] == 0:
                    x_grouped = x_work.tile([P, GROUP_WORK], BF16, align_bytes=64)
                    x_grouped_of[job, g] = x_grouped
                x_grouped_words = x_grouped_of[job, g][:].bitcast(F32)
                for bank in banks:
                    turned = turn_psum.tile([P, 2, 2, P], F32, tag="turn")
                    for s in range(2):
                        for u in range(2):
                            first = (g * RUN + 2 * bank + s) * (WIDTH // 2) + u * P
                            nc.tensor.transpose(
                                turned[:, s, u, :], x_words[:, first : first + P], ident_f32[:]
                            )
                    empty_bank(
                        bank in vector_banks,
                        x_grouped_words[:, bank * BANK : (bank + 1) * BANK].rearrange(
                            "p (s c u) -> p s c u", s=2, u=2
                        ),
                        turned[:].rearrange("p s u c -> p s c u"),
                    )

            def quantise_x(job, g):
                x_codes = x_mx.tile([P, BANK], U32, align_bytes=64)
                x_scales = x_mx.tile([P, BANK], U8, align_bytes=64)
                x_mx_of[job, g] = (x_codes, x_scales)
                nc.vector.quantize_mx(
                    out=x_codes[:].bitcast(FP8X4), scales=x_scales[:], in_=x_grouped_of[job, g][:]
                )

            def keep_warm(bank):
                nc.tensor.matmul(bank[:], lhsT=zeros[:, 0:P], rhs=zeros[:], start=True, stop=True)

            def pass_mx(q_acc, codes, scales, first, job, g, start, stop):
                x_codes, x_scales = x_mx_of[job, g]
                nc.tensor.matmul_mx(
                    out=q_acc[:],
                    lhsT=codes[:, first : first + P].bitcast(FP8X4),
                    lhsT_scale=scales[:, first : first + P],
                    rhs=x_codes[:].bitcast(FP8X4),
                    rhs_scale=x_scales[:],
                    start=start,
                    stop=stop,
                )

            def turn_bias(rows, first, count):
                bq_turned = acc_psum.tile([P, P], BF16, tag="acc")
                nc.tensor.transpose(bq_turned[:], rows[:], ident_bf16[:])
                nc.vector.tensor_scalar(
                    out=bias[:, first : first + count],
                    in0=bq_turned[:, 0:count],
                    scalar1=SCALING,
                    scalar2=None,
                    op0=ALU.mult,
                )

            def prepare_solo():
                for mixed, plain, width in (
                    (solo_codes[:].bitcast(I32), w_codes[:].bitcast(I32), HEAD_DIM),
                    (solo_scales[:].bitcast(I32), w_scales[:].bitcast(I32), HEAD_DIM // PACK),
                ):
                    nc.vector.tensor_copy(
                        out=mixed[:, 0 : 2 * HEADS * width].rearrange("p (h s w) -> p s h w", s=2, w=width)[:, 1],
                        in_=plain.rearrange("p (h w) -> p h w", w=width),
                    )
                turn_bias(bq_heads, PAIRS, HEADS)

            def project(job, units):
                for n, unit in enumerate(units):
                    g, pair = unit // PAIRS, unit % PAIRS
                    if pair == 0:
                        q_grouped = x_work.tile([P, PAIRS * BANK], BF16, align_bytes=64)
                        q_grouped_of[job, g] = q_grouped
                    q_grouped = q_grouped_of[job, g]
                    q_acc = acc_psum.tile([P, BANK], F32, tag="acc")
                    if job in SOLO:
                        h = 2 * pair + g
                        pass_mx(q_acc, solo_codes, solo_scales, (2 * h + 1) * HEAD_DIM, job, 0, True, False)
                        pass_mx(q_acc, solo_codes, solo_scales, 2 * h * HEAD_DIM, job, 1, False, True)
                        column = PAIRS + h
                    else:
                        if n < WARM:
                            keep_warm(q_acc)
                        pass_mx(q_acc, w_codes, w_scales, pair * P, job, g, True, True)
                        column = pair
                    nc.scalar.activation(
                        out=q_grouped[:, pair * BANK : (pair + 1) * BANK].rearrange(
                            "p (i t) -> p i t", t=PACK
                        ),
                        in_=q_acc[:].rearrange("p (t i) -> p i t", t=PACK),
                        func=ACT.Identity,
                        bias=bias[:, column : column + 1],
                        scale=SCALING,
                    )

            def quantise_q(job, g):
                it, half = job // HALVES, job % HALVES
                part = g if job in SOLO else 2 * g
                nc.vector.quantize_mx(
                    out=query_codes(it, part, range(half, half + 1)).bitcast(FP8X4),
                    scales=query_scales(it, part, range(half, half + 1)).bitcast(U8),
                    in_=q_grouped_of[job, g][:],
                )

            def regroup(its, moves):
                for move in moves:
                    for it in its:
                        halves = range(sum(it * HALVES + half not in SOLO for half in range(HALVES)))
                        for words in (query_codes, query_scales):
                            even, odd, both = (words(it, part, halves) for part in range(3))
                            if move == 0:
                                nc.sync.dma_start(out=odd[0:HEAD_DIM, :], in_=even[HEAD_DIM:P, :])
                            elif move == 1:
                                nc.sync.dma_start(out=odd[HEAD_DIM:P, :], in_=both[HEAD_DIM:P, :])
                            else:
                                nc.sync.dma_start(out=even[HEAD_DIM:P, :], in_=both[0:HEAD_DIM, :])

            def order_keys(job):
                k_by_head = k_order.tile([P, GROUPS * GROUP_WORK], BF16)
                k_by_head_of[job] = k_by_head
                nc.vector.tensor_copy(
                    out=k_by_head[:].rearrange("p (n g d) -> p n g d", g=GROUPS, d=HEAD_DIM),
                    in_=k_raw_of[job][:].rearrange("p (g n d) -> p n g d", g=GROUPS, d=HEAD_DIM),
                )

            def turn_keys(job, banks):
                if job % 2 == 0 and banks[0] == 0:
                    k_grouped = k_work.tile([P, 2 * GROUPS * GROUP_WORK], BF16, align_bytes=64)
                    k_grouped_of[job // 2] = k_grouped
                k_grouped = k_grouped_of[job // 2]
                k_grouped_words = k_grouped[:].bitcast(F32).rearrange(
                    "p (h n) -> p h n", h=HEADS
                )[:, :, job % 2 * 256 : (job % 2 + 1) * 256]
                k_by_head = k_by_head_of[job]
                for bank in banks:
                    turned = turn_psum.tile([P, 8, P], BF16, tag="turn")
                    for s in range(8):
                        h, b = 2 * bank + s // RUN, s % RUN
                        first = (b * HEADS + h) * P
                        nc.tensor.transpose(
                            turned[:, s, :], k_by_head[:, first : first + P], ident_bf16[:]
                        )
                    nc.scalar.copy(
                        out=k_grouped_words[:, 2 * bank : 2 * bank + 2, :],
                        in_=turned[:]
                        .rearrange("p s c -> p (s c)")
                        .bitcast(F32)
                        .rearrange("p (h n) -> p h n", h=2),
                    )

            def quantise_keys(job, part):
                first = ((job // 2) * HEADS + 4 * part) * KEY_SIDE
                nc.vector.quantize_mx(
                    out=k_codes[:, first : first + 4 * KEY_SIDE].bitcast(FP8X4),
                    scales=k_scales[:, first : first + 4 * KEY_SIDE],
                    in_=k_grouped_of[job // 2][:, part * 4096 : (part + 1) * 4096],
                )

            with tc.tile_pool(name="setup", bufs=1) as setup:
                load_x(0)
                load_rows(x_raw_of[0], 0, 0, 4)
                w_raw = setup.tile([P, PACK, WIDTH], BF16)
                nc.sync.dma_start(
                    out=w_raw[:].rearrange("p (u e) c -> p u (e c)", u=2),
                    in_=Wq.rearrange("(u p e) c -> p u (e c)", u=2, e=2),
                )
                bq_pairs = setup.tile([P, P], BF16)
                nc.vector.memset(bq_pairs[:], 0.0)
                nc.sync.dma_start(
                    out=bq_pairs[0:PAIRS, :], in_=bq.rearrange("(n f) -> n f", n=PAIRS)
                )
                load_rows(x_raw_of[0], 0, 4, 4)
                w_grouped = setup.tile([P, WIDTH * PACK], BF16, align_bytes=64)
                load_keys(0)
                load_x(1)
                load_keys(1)
                load_x(2)
                load_keys(2)
                nc.gpsimd.memset(bq_heads[:], 0.0)
                for half in range(2):
                    nc.sync.dma_start(
                        out=bq_heads[0:HEADS, half * HEAD_DIM : (half + 1) * HEAD_DIM],
                        in_=bq.rearrange("(h d) -> h d", h=HEADS),
                    )
                make_identity(nc, ident_f32[:])
                make_identity(nc, ident_bf16[:])
                nc.gpsimd.memset(
                    q_packed[:].rearrange("p (n w) -> p n w", w=2 * SIDE)[:, :, 2 * BANK :], 0
                )
                turn_x(0, 0, (1,))
                for half in range(2):
                    cols = slice(half * 256, (half + 1) * 256)
                    words = slice(half * 1024, (half + 1) * 1024)
                    empty_bank(
                        half == 0,
                        w_grouped[:, words].rearrange("p (c t) -> p c t", t=PACK),
                        w_raw[:, :, cols].rearrange("p t c -> p c t"),
                    )
                    nc.vector.quantize_mx(
                        out=w_codes[:, cols].bitcast(FP8X4), scales=w_scales[:, cols], in_=w_grouped[:, words]
                    )
                turn_bias(bq_pairs, 0, PAIRS)
                quantise_x(0, 0)
                turn_x(0, 1, (1,))
                project(0, (0, 1))
                quantise_x(0, 1)
                order_keys(0)

            solo = first_phase.enter_context(tc.tile_pool(name="solo", bufs=1))
            solo_codes = solo.tile([P, (2 * HEADS + 1) * HEAD_DIM], U32, align_bytes=64)
            solo_scales = solo.tile([P, (2 * HEADS + 1) * HEAD_DIM], U8, align_bytes=64)
            for step in range(X_JOBS):
                ahead = step + 1
                first_unit = 1 if step == 0 else 0
                if step + 3 < X_JOBS:
                    load_x(step + 3)
                if step + 3 < KEY_JOBS:
                    load_keys(step + 3)
                if step == LOADS_DONE:
                    regroup(range(0, 2), range(3))
                if step == X_JOBS - 1:
                    regroup(range(2, 3), range(3))
                if step == 1:
                    nc.gpsimd.memset(solo_codes[:].bitcast(I32), 0)
                    nc.gpsimd.memset(solo_scales[:].bitcast(I32), 0)
                if step == SOLO_STEP:
                    prepare_solo()
                for group in range(3):
                    units = UNITS[group] if step > 0 else FIRST_UNITS[group]
                    if step == 0:
                        project(step, units)
                    if ahead < X_JOBS:
                        if group == 0:
                            turn_x(ahead, 0, (0, 1))
                            turn_x(ahead, 1, (0, 1), (0,))
                        elif group == 1:
                            turn_x(ahead, 1, (0, 1), (1,))
                        key_banks = ((), (0, 1), (2, 3))[group]
                    else:
                        key_banks = ((0, 1, 2), (3,), ())[group]
                    if key_banks:
                        turn_keys(step, key_banks)
                    if step > 0:
                        project(step, units)
                    if group == 0:
                        if step >= 1:
                            quantise_q(step - 1, 1)
                        if ahead < X_JOBS:
                            quantise_x(ahead, 0)
                        if step % 2 == 0 and step >= 2:
                            quantise_keys(step - 1, 0)
                    if group == 1:
                        if step + 1 < KEY_JOBS:
                            order_keys(step + 1)
                        if ahead == X_JOBS:
                            quantise_keys(step, 0)
                    if group == 2:
                        quantise_q(step, 0)
                        if ahead < X_JOBS:
                            quantise_x(ahead, 1)
                        if step % 2 == 0 and step >= 2:
                            quantise_keys(step - 1, 1)
                        if ahead == X_JOBS:
                            quantise_keys(step, 1)
            quantise_q(X_JOBS - 1, 1)
            regroup(range(3, 4), range(3))

        probs_pool = ctx.enter_context(tc.tile_pool(name="probs_pool", bufs=12))
        soft = ctx.enter_context(tc.tile_pool(name="soft", bufs=8))
        scores_of, probs_of, total_of = {}, {}, {}

        def attend_scores(n):
            it, h = n // HEADS, n % HEADS
            scores = acc_psum.tile([P, COLS], F32, tag="acc")
            for side, half in ((0, 0), (0, 1), (1, 0), (1, 1)):
                q_codes = query_codes(it, h % 2, range(half, half + 1))
                q_scales = query_scales(it, h % 2, range(half, half + 1)).bitcast(U8)
                q_first = (h // 2) * P
                k_first = ((half * 2 + side) * HEADS + h) * KEY_SIDE
                nc.tensor.matmul_mx(
                    out=scores[:, side * KEY_SIDE : (side + 1) * KEY_SIDE],
                    lhsT=q_codes[:, q_first : q_first + P].bitcast(FP8X4),
                    lhsT_scale=q_scales[:, q_first : q_first + P],
                    rhs=k_codes[:, k_first : k_first + KEY_SIDE].bitcast(FP8X4),
                    rhs_scale=k_scales[:, k_first : k_first + KEY_SIDE],
                    start=(half == 0),
                    stop=(half == HALVES - 1),
                )
            neg_max = soft.tile([P, 1], F32)
            nc.vector.tensor_reduce(
                out=neg_max[:], in_=scores[:], axis=mybir.AxisListType.X, op=ALU.max, negate=True
            )
            scores_of[n] = (scores, neg_max)

        def attend_exp(n):
            scores, neg_max = scores_of[n]
            probs = probs_pool.tile([P, COLS], F32)
            if n % 2 == 0:
                total = soft.tile([P, 2], F32)
                total_of[n // 2] = total
            nc.scalar.activation(
                out=probs[:].rearrange("p (tile c b) -> p tile c b", b=RUN, tile=COL_TILES),
                in_=scores[:].rearrange("p (tile b c) -> p tile c b", b=RUN, tile=COL_TILES),
                func=ACT.Exp,
                bias=neg_max[:, 0:1],
                scale=1.0,
                accum_out=total_of[n // 2][:, n % 2 : n % 2 + 1],
            )
            probs_of[n] = probs

        def attend_inverse(pair):
            inverse = soft.tile([P, 2], F32)
            nc.vector.reciprocal(out=inverse[:], in_=total_of[pair][:])
            total_of[pair] = inverse

        def attend_normalise(pair):
            inverse = total_of[pair]
            for n in (2 * pair, 2 * pair + 1):
                probs, factor = probs_of[n], inverse[:, n % 2 : n % 2 + 1]
                if n % 8 == 7:
                    nc.scalar.activation(out=probs[:], in_=probs[:], func=ACT.Copy, scale=factor)
                else:
                    engine = nc.gpsimd
                    engine.tensor_scalar(
                        out=probs[:], in0=probs[:], scalar1=factor, scalar2=0.0,
                        op0=ALU.mult, op1=ALU.add,
                    )

        def attend_store(n):
            it, h = n // HEADS, n % HEADS
            nc.sync.dma_start(out=out_view[:, h, it, :], in_=probs_of[n][:])

        for n in range(MAPS + STORE_LAG):
            if n < MAPS:
                attend_scores(n)
            if 1 <= n <= MAPS:
                attend_exp(n - 1)
            if 3 <= n <= MAPS + 2 and n % 2 == 1:
                attend_inverse((n - 3) // 2)
            if 4 <= n <= MAPS + 3 and n % 2 == 0:
                attend_normalise((n - 4) // 2)
            if n >= STORE_LAG:
                attend_store(n - STORE_LAG)
